import numpy as np
import ml_dtypes


def mxq(x, axis, fmt="e4m3"):
    dtype, down = {"e4m3": (ml_dtypes.float8_e4m3fn, 7), "e5m2": (ml_dtypes.float8_e5m2, 14)}[fmt]
    v = np.moveaxis(np.asarray(x, np.float32).astype(ml_dtypes.bfloat16).astype(np.float64), axis, -1)
    blocks = v.reshape(v.shape[:-1] + (-1, 32))
    amax = np.abs(blocks).max(-1, keepdims=True)
    byte = np.maximum(np.where(amax > 0, np.frexp(amax)[1] - 1 + 127, 0) - down, 1)
    scale = np.exp2(byte - 127.0)
    codes = (blocks / scale).astype(np.float32).astype(dtype).astype(np.float64)
    return np.moveaxis((codes * scale).reshape(v.shape), -1, axis)


WIDE = False


def mx_kscale(k):
    if not WIDE:
        return np.ones(k)
    levels = np.array([10, -10, 5, -5, 0])
    a = np.random.permutation(np.resize(levels, k // 512 * 4)).reshape(k // 512, 4)
    idx = np.arange(k)
    return np.exp2(a[idx // 512, idx % 128 // 32])


BF16 = ml_dtypes.bfloat16


def bf(x):
    return np.asarray(x, np.float32).astype(BF16)


def f64(x):
    return np.asarray(x).astype(np.float64)


E2M1 = np.array([0.0, 0.5, 1.0, 1.5, 2.0, 3.0, 4.0, 6.0, -0.0, -0.5, -1.0, -1.5, -2.0, -3.0, -4.0, -6.0])


def pack_weight(w, fmt):
    k, n = w.shape
    w = f64(bf(w)).reshape(k // 32, 32, n)
    amax = np.abs(w).max(1)
    if fmt == "e4m3":
        byte = np.frexp(amax)[1] - 1 + 127 - 7
    else:
        mant, ex = np.frexp(amax / 6.0)
        byte = np.where(mant > 0.5, ex, ex - 1) + 127
    byte = np.clip(np.where(amax > 0, byte, 1), 1, 254)
    scaled = (w * np.exp2(127.0 - byte)[:, None, :]).reshape(k, n).astype(np.float32)
    by_word = np.ascontiguousarray(scaled.reshape(k // 512, 128, 4, n).transpose(0, 1, 3, 2))
    if fmt == "e4m3":
        words = by_word.astype(ml_dtypes.float8_e4m3fn).view(np.uint8)
    else:
        c = by_word.astype(ml_dtypes.float4_e2m1fn).view(np.uint8) & 0xF
        words = c[..., 0::2] | (c[..., 1::2] << 4)
    return np.ascontiguousarray(words), np.ascontiguousarray(byte.astype(np.uint8).reshape(k // 512, 16, n))


def unpack_weight(words, scales, fmt):
    g, p, n, _ = words.shape
    if fmt == "e4m3":
        vals = np.ascontiguousarray(words).view(ml_dtypes.float8_e4m3fn).astype(np.float64)
    else:
        nib = np.empty((g, p, n, 4), np.uint8)
        nib[..., 0::2] = words & 0xF
        nib[..., 1::2] = words >> 4
        vals = E2M1[nib]
    vals = vals * np.repeat(np.exp2(scales.astype(np.float64) - 127.0), 8, axis=1)[..., None]
    return vals.transpose(0, 1, 3, 2).reshape(g * 512, n)


B, N, C = 64, 16, 512
NEG_SLOPE = 0.2
FMT = "e4m3"


def leaky(v):
    return np.where(v >= 0, v, NEG_SLOPE * v)


def setup_inputs():
    s, t = mx_kscale(C), mx_kscale(C)
    w1 = np.random.standard_normal((2, C, C)) * 0.7 / np.sqrt(C) / s[None, :, None] * t
    F = bf(np.random.standard_normal((B, N, C)) * s)
    W1_words, W1_scales = pack_weight(w1.reshape(2 * C, C), FMT)
    b1 = bf(np.random.standard_normal(C) * 0.2 * t)
    W2_words, W2_scales = pack_weight(np.random.standard_normal((C, C)) / np.sqrt(C) / t[:, None], FMT)
    b2 = bf(np.random.standard_normal(C) * 0.2)
    return {"F": F,
            "W1_words": W1_words,
            "W1_scales": W1_scales,
            "b1": b1,
            "W2_words": W2_words,
            "W2_scales": W2_scales,
            "b2": b2}


def reference(F, W1_words, W1_scales, b1, W2_words, W2_scales, b2):
    Fq = mxq(f64(F), 2, "e4m3")
    W1 = unpack_weight(W1_words, W1_scales, FMT)
    W2 = unpack_weight(W2_words, W2_scales, FMT)
    A = Fq @ W1[:C]
    Bp = Fq @ W1[C:]
    h = leaky(A[:, :, None, :] + Bp[:, None, :, :] + f64(b1))
    h = leaky((mxq(h, 3, "e4m3") @ W2) + f64(b2))
    return h.sum(-2)

@@ -1,0 +1,236 @@
+from contextlib import ExitStack
+
+import concourse.mybir as mybir
+from concourse.masks import make_identity
+
+F32 = mybir.dt.float32
+BF16 = mybir.dt.bfloat16
+I32 = mybir.dt.int32
+U32 = mybir.dt.uint32
+U8 = mybir.dt.uint8
+FP8X4 = mybir.dt.float8_e4m3fn_x4
+ALU = mybir.AluOpType
+ACT = mybir.ActivationFunctionType
+
+P = 128
+PACK = 4
+SETS, NODES, C = 64, 16, 512
+ROWS = SETS * NODES
+ROW_TILES = ROWS // P
+HALVES = 2
+HALF_ROWS = ROWS // HALVES
+HALF_SETS = SETS // HALVES
+HALF_TILES = ROW_TILES // HALVES
+OUT_TILES = C // P
+NEG_SLOPE = 0.2
+LEAD = 2
+
+FLOPS = 2 * ROWS * (2 * C) * C + 2 * SETS * NODES * NODES * C * C
+
+
+def tile_nonlocalmp_pa_t_kernel(tc, F, W1_words, W1_scales, b1, W2_words, W2_scales, b2, out):
+    nc = tc.nc
+    f_rows = F.flatten_outer_dims()
+    out_rows = out.flatten_outer_dims()
+
+    with ExitStack() as ctx:
+        keep = ctx.enter_context(tc.tile_pool(name="keep", bufs=1))
+        stage = ctx.enter_context(tc.tile_pool(name="stage", bufs=4))
+        pairs = ctx.enter_context(tc.tile_pool(name="pairs", bufs=3))
+        sums = ctx.enter_context(tc.tile_pool(name="sums", bufs=2))
+        psum = ctx.enter_context(tc.psum_pool(name="psum", bufs=4))
+
+        w_planes = keep.tile([P, 3, C], U8, align_bytes=64)
+        nc.vector.memset(w_planes[:].rearrange("p g n -> p (g n)").bitcast(I32), 0)
+
+        f_sb = keep.tile([P, ROW_TILES, C], BF16)
+        for hf in range(HALVES):
+            nc.sync.dma_start(
+                out=f_sb[:, hf * HALF_TILES : (hf + 1) * HALF_TILES, :],
+                in_=f_rows[hf * HALF_ROWS : (hf + 1) * HALF_ROWS, :].rearrange("(a p) c -> p a c", p=P),
+            )
+        for quad in range(4):
+            nc.sync.dma_start(
+                out=w_planes[32 * quad : 32 * quad + 4, 0:2, :].bitcast(I32),
+                in_=W1_scales[:, 4 * quad : 4 * quad + 4, :].rearrange("g r n -> r g n").bitcast(I32),
+            )
+        w1 = keep.tile([P, 2, C], U32, align_bytes=64)
+        nc.sync.dma_start(out=w1[:].bitcast(I32), in_=W1_words.rearrange("g p n t -> p g (n t)").bitcast(I32))
+        for quad in range(4):
+            nc.sync.dma_start(
+                out=w_planes[32 * quad : 32 * quad + 4, 2, :].bitcast(I32),
+                in_=W2_scales[0, 4 * quad : 4 * quad + 4, :].bitcast(I32),
+            )
+        w2 = keep.tile([P, C], U32, align_bytes=64)
+        nc.sync.dma_start(out=w2[:].bitcast(I32), in_=W2_words[0].rearrange("p n t -> p (n t)").bitcast(I32))
+
+        b1_pt = keep.tile([P, PACK], BF16)
+        nc.scalar.dma_start(out=b1_pt[:], in_=b1.rearrange("(p t) -> p t", t=PACK))
+        b2_rows = keep.tile([P, P], BF16)
+        nc.vector.memset(b2_rows[:], 0.0)
+        nc.scalar.dma_start(out=b2_rows[0:OUT_TILES, :], in_=b2.rearrange("(n p) -> n p", p=P))
+
+        ident = keep.tile([P, P], F32)
+        make_identity(nc, ident[:])
+
+        b2_square = keep.tile([P, P], F32)
+        nc.vector.tensor_copy(out=b2_square[:], in_=b2_rows[:])
+        b2_ps = psum.tile([P, C], F32, tag="work")
+        nc.tensor.transpose(b2_ps[:, 0:P], b2_square[:], ident[:])
+        neg_b2 = keep.tile([P, OUT_TILES], F32)
+        nc.vector.tensor_scalar(out=neg_b2[:], in0=b2_ps[:, 0:OUT_TILES], scalar1=-1.0, scalar2=None, op0=ALU.mult)
+        b2_x16 = keep.tile([P, OUT_TILES], F32)
+        nc.vector.tensor_scalar(
+            out=b2_x16[:], in0=b2_ps[:, 0:OUT_TILES], scalar1=float(NODES), scalar2=None, op0=ALU.mult
+        )
+
+        f_grp = keep.tile([P, ROWS, PACK], BF16, align_bytes=64)
+        f_grp_words = f_grp[:].rearrange("p r t -> p (r t)").bitcast(F32).rearrange("p (r u) -> p r u", u=2)
+        f_codes = keep.tile([P, ROWS], U32, align_bytes=64)
+        f_scales = keep.tile([P, ROWS], U8, align_bytes=64)
+        for a in range(ROW_TILES):
+            f_words = f_sb[:, a, :].bitcast(F32)
+            f_ps = psum.tile([P, C], F32, tag="work")
+            for u in range(2):
+                nc.tensor.transpose(f_ps[:, u * P : (u + 1) * P], f_words[:, u : C // 2 : 2], ident[:])
+            nc.vector.tensor_copy(
+                out=f_grp_words[:, a * P : (a + 1) * P, :],
+                in_=f_ps[:, 0 : 2 * P].rearrange("p (u r) -> p r u", u=2),
+            )
+        for hf in range(HALVES):
+            half = slice(hf * HALF_ROWS, (hf + 1) * HALF_ROWS)
+            nc.vector.quantize_mx(
+                out=f_codes[:, half].bitcast(FP8X4),
+                scales=f_scales[:, half],
+                in_=f_grp[:, half, :].rearrange("p r t -> p (r t)"),
+            )
+
+        a_t = keep.tile([P, ROWS, PACK], F32)
+        b_t = keep.tile([P, ROWS, PACK], F32)
+        for a in range(ROW_TILES):
+            rows = slice(a * P, (a + 1) * P)
+            for g in range(2):
+                prod = psum.tile([P, C], F32, tag="work")
+                nc.tensor.matmul_mx(
+                    out=prod[:],
+                    lhsT=f_codes[:, rows].bitcast(FP8X4),
+                    lhsT_scale=f_scales[:, rows],
+                    rhs=w1[:, g, :].bitcast(FP8X4),
+                    rhs_scale=w_planes[:, g, :],
+                    start=True,
+                    stop=True,
+                )
+                sorted_ch = stage.tile([P, PACK, P], F32)
+                nc.scalar.copy(out=sorted_ch[:], in_=prod[:].rearrange("r (m t) -> r t m", t=PACK))
+                turned = psum.tile([P, C], F32, tag="work")
+                for t in range(PACK):
+                    nc.tensor.transpose(turned[:, t * P : (t + 1) * P], sorted_ch[:, t, :], ident[:])
+                turned_rt = turned[:].rearrange("p (t r) -> p r t", t=PACK)
+                if g == 0:
+                    nc.scalar.copy(out=a_t[:, rows, :], in_=turned_rt)
+                else:
+                    nc.vector.tensor_tensor(
+                        out=b_t[:, rows, :],
+                        in0=turned_rt,
+                        in1=b1_pt[:].unsqueeze(1).to_broadcast([P, P, PACK]),
+                        op=ALU.add,
+                    )
+
+        steps = [(hf, j) for hf in range(HALVES) for j in range(NODES)]
+        v_bf, w_bf = {}, {}
+        acc, lin = {}, {}
+
+        def add_pairs(s):
+            hf, j = steps[s]
+            half = slice(hf * HALF_ROWS, (hf + 1) * HALF_ROWS)
+            v = pairs.tile([P, HALF_ROWS, PACK], F32, name="v", tag="v")
+            nc.vector.tensor_tensor(
+                out=v[:].rearrange("p (b i) t -> p b i t", i=NODES),
+                in0=a_t[:, half, :].rearrange("p (b i) t -> p b i t", i=NODES),
+                in1=b_t[:, half, :]
+                .rearrange("p (b i) t -> p b i t", i=NODES)[:, :, j : j + 1, :]
+                .to_broadcast([P, HALF_SETS, NODES, PACK]),
+                op=ALU.add,
+            )
+            v_flat = v[:].rearrange("p c t -> p (c t)")
+            v_bf[s] = pairs.tile([P, HALF_ROWS * PACK], BF16, name="v_bf", tag="v_bf")
+            w_bf[s] = pairs.tile([P, HALF_ROWS * PACK], BF16, name="w_bf", tag="w_bf")
+            nc.scalar.copy(out=v_bf[s][:], in_=v_flat)
+            nc.scalar.mul(out=w_bf[s][:], in_=v_flat, mul=NEG_SLOPE)
+
+        def multiply(s):
+            hf, j = steps[s]
+            h = pairs.tile([P, HALF_ROWS * PACK], BF16, name="h", tag="h", align_bytes=64)
+            nc.vector.tensor_tensor(out=h[:], in0=v_bf[s][:], in1=w_bf[s][:], op=ALU.max)
+            h_codes = pairs.tile([P, HALF_ROWS], U32, name="h_codes", tag="h_codes", align_bytes=64)
+            h_scales = pairs.tile([P, HALF_ROWS], U8, name="h_scales", tag="h_scales", align_bytes=64)
+            nc.vector.quantize_mx(out=h_codes[:].bitcast(FP8X4), scales=h_scales[:], in_=h[:])
+            if j == 0:
+                lin[hf] = [psum.tile([P, HALF_ROWS], F32, name="lin%d" % n, tag="lin") for n in range(OUT_TILES)]
+            x = []
+            for n in range(OUT_TILES):
+                cols = slice(n * P, (n + 1) * P)
+                x.append(psum.tile([P, HALF_ROWS], F32, name="x%d" % n, tag="work"))
+                for target, first, last in ((x[n], True, True), (lin[hf][n], j == 0, j == NODES - 1)):
+                    nc.tensor.matmul_mx(
+                        out=target[:],
+                        lhsT=w2[:, cols].bitcast(FP8X4),
+                        lhsT_scale=w_planes[:, 2, cols],
+                        rhs=h_codes[:].bitcast(FP8X4),
+                        rhs_scale=h_scales[:],
+                        start=first,
+                        stop=last,
+                    )
+            return x
+
+        def accumulate(s, x):
+            hf, j = steps[s]
+            if j == 0:
+                acc[hf] = sums.tile([P, OUT_TILES, HALF_ROWS], F32, name="acc", tag="acc")
+            for n in range(OUT_TILES):
+                if j == 0:
+                    nc.vector.tensor_scalar(
+                        out=acc[hf][:, n, :], in0=x[n][:], scalar1=neg_b2[:, n : n + 1], scalar2=None, op0=ALU.max
+                    )
+                else:
+                    nc.vector.scalar_tensor_tensor(
+                        out=acc[hf][:, n, :],
+                        in0=x[n][:],
+                        scalar=neg_b2[:, n : n + 1],
+                        in1=acc[hf][:, n, :],
+                        op0=ALU.max,
+                        op1=ALU.add,
+                    )
+
+        def finish(hf):
+            for n in range(OUT_TILES):
+                base = sums.tile([P, HALF_ROWS], F32, name="base", tag="base")
+                nc.scalar.activation(
+                    out=base[:], in_=lin[hf][n][:], func=ACT.Identity, bias=b2_x16[:, n : n + 1], scale=NEG_SLOPE
+                )
+                nc.vector.scalar_tensor_tensor(
+                    out=acc[hf][:, n, :],
+                    in0=acc[hf][:, n, :],
+                    scalar=1.0 - NEG_SLOPE,
+                    in1=base[:],
+                    op0=ALU.mult,
+                    op1=ALU.add,
+                )
+            for a in range(HALF_TILES):
+                back = psum.tile([P, C], F32, name="back", tag="work")
+                for n in range(OUT_TILES):
+                    nc.tensor.transpose(back[:, n * P : (n + 1) * P], acc[hf][:, n, a * P : (a + 1) * P], ident[:])
+                result = stage.tile([P, C], F32, name="result", tag="result")
+                nc.scalar.copy(out=result[:], in_=back[:])
+                first_row = hf * HALF_ROWS + a * P
+                nc.sync.dma_start(out=out_rows[first_row : first_row + P, :], in_=result[:])
+
+        for s in range(LEAD):
+            add_pairs(s)
+        for s in range(len(steps)):
+            x = multiply(s)
+            if s + LEAD < len(steps):
+                add_pairs(s + LEAD)
+            accumulate(s, x)
+            if steps[s][1] == NODES - 1:
+                finish(steps[s][0])

@@ -17,13 +17,16 @@ PACK = 4
 SETS, NODES, C = 64, 16, 512
 ROWS = SETS * NODES
 ROW_TILES = ROWS // P
-HALVES = 2
-HALF_ROWS = ROWS // HALVES
-HALF_SETS = SETS // HALVES
-HALF_TILES = ROW_TILES // HALVES
+TILE_SETS = P // NODES
+J_STEP = 4
+STEPS_PER_TILE = NODES // J_STEP
+COLS = J_STEP * P
 OUT_TILES = C // P
 NEG_SLOPE = 0.2
+POS_SLOPE = 1.0 - NEG_SLOPE
+SCALAR_COLS = COLS // 2
 LEAD = 2
+AHEAD = 2
 
 FLOPS = 2 * ROWS * (2 * C) * C + 2 * SETS * NODES * NODES * C * C
 
@@ -37,18 +40,16 @@ def tile_nonlocalmp_pa_t_kernel(tc, F, W1_words, W1_scales, b1, W2_words, W2_sca
         keep = ctx.enter_context(tc.tile_pool(name="keep", bufs=1))
         stage = ctx.enter_context(tc.tile_pool(name="stage", bufs=4))
         pairs = ctx.enter_context(tc.tile_pool(name="pairs", bufs=3))
-        sums = ctx.enter_context(tc.tile_pool(name="sums", bufs=2))
-        psum = ctx.enter_context(tc.psum_pool(name="psum", bufs=4))
+        relus = ctx.enter_context(tc.tile_pool(name="relus", bufs=2 * OUT_TILES))
+        banks = ctx.enter_context(tc.psum_pool(name="banks", bufs=4))
+        groups = ctx.enter_context(tc.psum_pool(name="groups", bufs=2))
 
         w_planes = keep.tile([P, 3, C], U8, align_bytes=64)
         nc.vector.memset(w_planes[:].rearrange("p g n -> p (g n)").bitcast(I32), 0)
 
         f_sb = keep.tile([P, ROW_TILES, C], BF16)
-        for hf in range(HALVES):
-            nc.sync.dma_start(
-                out=f_sb[:, hf * HALF_TILES : (hf + 1) * HALF_TILES, :],
-                in_=f_rows[hf * HALF_ROWS : (hf + 1) * HALF_ROWS, :].rearrange("(a p) c -> p a c", p=P),
-            )
+        f_tiled = f_rows.rearrange("(a p) c -> p a c", p=P)
+        nc.sync.dma_start(out=f_sb[:, 0:AHEAD, :], in_=f_tiled[:, 0:AHEAD, :])
         for quad in range(4):
             nc.sync.dma_start(
                 out=w_planes[32 * quad : 32 * quad + 4, 0:2, :].bitcast(I32),
@@ -63,6 +64,7 @@ def tile_nonlocalmp_pa_t_kernel(tc, F, W1_words, W1_scales, b1, W2_words, W2_sca
             )
         w2 = keep.tile([P, C], U32, align_bytes=64)
         nc.sync.dma_start(out=w2[:].bitcast(I32), in_=W2_words[0].rearrange("p n t -> p (n t)").bitcast(I32))
+        nc.sync.dma_start(out=f_sb[:, AHEAD:ROW_TILES, :], in_=f_tiled[:, AHEAD:ROW_TILES, :])
 
         b1_pt = keep.tile([P, PACK], BF16)
         nc.scalar.dma_start(out=b1_pt[:], in_=b1.rearrange("(p t) -> p t", t=PACK))
@@ -73,44 +75,33 @@ def tile_nonlocalmp_pa_t_kernel(tc, F, W1_words, W1_scales, b1, W2_words, W2_sca
         ident = keep.tile([P, P], F32)
         make_identity(nc, ident[:])
 
-        b2_square = keep.tile([P, P], F32)
-        nc.vector.tensor_copy(out=b2_square[:], in_=b2_rows[:])
-        b2_ps = psum.tile([P, C], F32, tag="work")
-        nc.tensor.transpose(b2_ps[:, 0:P], b2_square[:], ident[:])
-        neg_b2 = keep.tile([P, OUT_TILES], F32)
-        nc.vector.tensor_scalar(out=neg_b2[:], in0=b2_ps[:, 0:OUT_TILES], scalar1=-1.0, scalar2=None, op0=ALU.mult)
-        b2_x16 = keep.tile([P, OUT_TILES], F32)
-        nc.vector.tensor_scalar(
-            out=b2_x16[:], in0=b2_ps[:, 0:OUT_TILES], scalar1=float(NODES), scalar2=None, op0=ALU.mult
-        )
-
         f_grp = keep.tile([P, ROWS, PACK], BF16, align_bytes=64)
         f_grp_words = f_grp[:].rearrange("p r t -> p (r t)").bitcast(F32).rearrange("p (r u) -> p r u", u=2)
         f_codes = keep.tile([P, ROWS], U32, align_bytes=64)
         f_scales = keep.tile([P, ROWS], U8, align_bytes=64)
-        for a in range(ROW_TILES):
+        a_t = keep.tile([P, ROW_TILES, P, PACK], F32)
+        b_t = keep.tile([P, ROW_TILES, NODES, TILE_SETS, PACK], F32)
+        sorted_ch = {}
+
+        def prepare_codes(a):
+            rows = slice(a * P, (a + 1) * P)
             f_words = f_sb[:, a, :].bitcast(F32)
-            f_ps = psum.tile([P, C], F32, tag="work")
+            f_ps = banks.tile([P, C], F32, name="f_ps", tag="bank")
             for u in range(2):
                 nc.tensor.transpose(f_ps[:, u * P : (u + 1) * P], f_words[:, u : C // 2 : 2], ident[:])
             nc.vector.tensor_copy(
-                out=f_grp_words[:, a * P : (a + 1) * P, :],
-                in_=f_ps[:, 0 : 2 * P].rearrange("p (u r) -> p r u", u=2),
+                out=f_grp_words[:, rows, :], in_=f_ps[:, 0 : 2 * P].rearrange("p (u r) -> p r u", u=2)
             )
-        for hf in range(HALVES):
-            half = slice(hf * HALF_ROWS, (hf + 1) * HALF_ROWS)
             nc.vector.quantize_mx(
-                out=f_codes[:, half].bitcast(FP8X4),
-                scales=f_scales[:, half],
-                in_=f_grp[:, half, :].rearrange("p r t -> p (r t)"),
+                out=f_codes[:, rows].bitcast(FP8X4),
+                scales=f_scales[:, rows],
+                in_=f_grp[:, rows, :].rearrange("p r t -> p (r t)"),
             )
 
-        a_t = keep.tile([P, ROWS, PACK], F32)
-        b_t = keep.tile([P, ROWS, PACK], F32)
-        for a in range(ROW_TILES):
+        def prepare_products(a):
             rows = slice(a * P, (a + 1) * P)
             for g in range(2):
-                prod = psum.tile([P, C], F32, tag="work")
+                prod = banks.tile([P, C], F32, name="prod", tag="bank")
                 nc.tensor.matmul_mx(
                     out=prod[:],
                     lhsT=f_codes[:, rows].bitcast(FP8X4),
@@ -120,117 +111,170 @@ def tile_nonlocalmp_pa_t_kernel(tc, F, W1_words, W1_scales, b1, W2_words, W2_sca
                     start=True,
                     stop=True,
                 )
-                sorted_ch = stage.tile([P, PACK, P], F32)
-                nc.scalar.copy(out=sorted_ch[:], in_=prod[:].rearrange("r (m t) -> r t m", t=PACK))
-                turned = psum.tile([P, C], F32, tag="work")
-                for t in range(PACK):
-                    nc.tensor.transpose(turned[:, t * P : (t + 1) * P], sorted_ch[:, t, :], ident[:])
-                turned_rt = turned[:].rearrange("p (t r) -> p r t", t=PACK)
+                sorted_ch[a, g] = stage.tile([P, PACK, P], F32, name="sorted_ch", tag="sorted_ch")
+                by_t = prod[:].rearrange("r (m t) -> r t m", t=PACK)
                 if g == 0:
-                    nc.scalar.copy(out=a_t[:, rows, :], in_=turned_rt)
+                    nc.scalar.copy(out=sorted_ch[a, g][:], in_=by_t)
+                else:
+                    nc.vector.tensor_copy(out=sorted_ch[a, g][:], in_=by_t)
+
+        def prepare_turned(a):
+            for g in range(2):
+                turned = banks.tile([P, C], F32, name="turned", tag="bank")
+                for t in range(PACK):
+                    nc.tensor.transpose(turned[:, t * P : (t + 1) * P], sorted_ch[a, g][:, t, :], ident[:])
+                if g == 0:
+                    nc.scalar.copy(out=a_t[:, a], in_=turned[:].rearrange("p (t r) -> p r t", t=PACK))
                 else:
                     nc.vector.tensor_tensor(
-                        out=b_t[:, rows, :],
-                        in0=turned_rt,
-                        in1=b1_pt[:].unsqueeze(1).to_broadcast([P, P, PACK]),
+                        out=b_t[:, a],
+                        in0=turned[:].rearrange("p (t b j) -> p j b t", t=PACK, j=NODES),
+                        in1=b1_pt[:].unsqueeze(1).unsqueeze(1).to_broadcast([P, NODES, TILE_SETS, PACK]),
                         op=ALU.add,
                     )
 
-        steps = [(hf, j) for hf in range(HALVES) for j in range(NODES)]
-        v_bf, w_bf = {}, {}
-        acc, lin = {}, {}
+        for phase in (prepare_codes, prepare_products, prepare_turned):
+            for a in range(AHEAD):
+                phase(a)
+
+        b2_square = keep.tile([P, P], F32)
+        nc.vector.tensor_copy(out=b2_square[:], in_=b2_rows[:])
+        b2_ps = banks.tile([P, C], F32, name="b2_ps", tag="bank")
+        nc.tensor.transpose(b2_ps[:, 0:P], b2_square[:], ident[:])
+        b2_pos = keep.tile([P, OUT_TILES], F32)
+        nc.vector.tensor_scalar(out=b2_pos[:], in0=b2_ps[:, 0:OUT_TILES], scalar1=POS_SLOPE, scalar2=None, op0=ALU.mult)
+        b2_sum = keep.tile([P, OUT_TILES], F32)
+        nc.vector.tensor_scalar(
+            out=b2_sum[:], in0=b2_ps[:, 0:OUT_TILES], scalar1=NODES * NEG_SLOPE, scalar2=None, op0=ALU.mult
+        )
+        b2_squares = keep.tile([P, OUT_TILES, P], F32)
+        nc.vector.tensor_copy(out=b2_squares[:], in_=b2_sum[:].unsqueeze(2).to_broadcast([P, OUT_TILES, P]))
+
+        steps = [(a, q) for a in range(ROW_TILES) for q in range(STEPS_PER_TILE)]
+        h, v_bf, w_bf = {}, {}, {}
+        lin, pos = {}, {}
 
         def add_pairs(s):
-            hf, j = steps[s]
-            half = slice(hf * HALF_ROWS, (hf + 1) * HALF_ROWS)
-            v = pairs.tile([P, HALF_ROWS, PACK], F32, name="v", tag="v")
+            a, q = steps[s]
+            shape = [P, J_STEP, TILE_SETS, NODES, PACK]
+            v = pairs.tile([P, COLS * PACK], F32, name="v", tag="v")
             nc.vector.tensor_tensor(
-                out=v[:].rearrange("p (b i) t -> p b i t", i=NODES),
-                in0=a_t[:, half, :].rearrange("p (b i) t -> p b i t", i=NODES),
-                in1=b_t[:, half, :]
-                .rearrange("p (b i) t -> p b i t", i=NODES)[:, :, j : j + 1, :]
-                .to_broadcast([P, HALF_SETS, NODES, PACK]),
+                out=v[:].rearrange("p (j b i t) -> p j b i t", j=J_STEP, b=TILE_SETS, i=NODES),
+                in0=a_t[:, a].rearrange("p (b i) t -> p b i t", i=NODES).unsqueeze(1).to_broadcast(shape),
+                in1=b_t[:, a, q * J_STEP : (q + 1) * J_STEP].unsqueeze(3).to_broadcast(shape),
                 op=ALU.add,
             )
-            v_flat = v[:].rearrange("p c t -> p (c t)")
-            v_bf[s] = pairs.tile([P, HALF_ROWS * PACK], BF16, name="v_bf", tag="v_bf")
-            w_bf[s] = pairs.tile([P, HALF_ROWS * PACK], BF16, name="w_bf", tag="w_bf")
-            nc.scalar.copy(out=v_bf[s][:], in_=v_flat)
-            nc.scalar.mul(out=w_bf[s][:], in_=v_flat, mul=NEG_SLOPE)
+            split = SCALAR_COLS * PACK
+            h[s] = pairs.tile([P, COLS * PACK], BF16, name="h", tag="h", align_bytes=64)
+            nc.vector.scalar_tensor_tensor(
+                out=h[s][:, split:], in0=v[:, split:], scalar=NEG_SLOPE, in1=v[:, split:], op0=ALU.mult, op1=ALU.max
+            )
+            return v
 
-        def multiply(s):
-            hf, j = steps[s]
-            h = pairs.tile([P, HALF_ROWS * PACK], BF16, name="h", tag="h", align_bytes=64)
-            nc.vector.tensor_tensor(out=h[:], in0=v_bf[s][:], in1=w_bf[s][:], op=ALU.max)
-            h_codes = pairs.tile([P, HALF_ROWS], U32, name="h_codes", tag="h_codes", align_bytes=64)
-            h_scales = pairs.tile([P, HALF_ROWS], U8, name="h_scales", tag="h_scales", align_bytes=64)
-            nc.vector.quantize_mx(out=h_codes[:].bitcast(FP8X4), scales=h_scales[:], in_=h[:])
-            if j == 0:
-                lin[hf] = [psum.tile([P, HALF_ROWS], F32, name="lin%d" % n, tag="lin") for n in range(OUT_TILES)]
+        def round_pairs(s, v):
+            split = SCALAR_COLS * PACK
+            v_bf[s] = pairs.tile([P, split], BF16, name="v_bf", tag="v_bf")
+            w_bf[s] = pairs.tile([P, split], BF16, name="w_bf", tag="w_bf")
+            nc.scalar.copy(out=v_bf[s][:], in_=v[:, 0:split])
+            nc.scalar.mul(out=w_bf[s][:], in_=v[:, 0:split], mul=NEG_SLOPE)
+
+        def quantise(s):
+            split = SCALAR_COLS * PACK
+            nc.vector.tensor_tensor(out=h[s][:, 0:split], in0=v_bf[s][:], in1=w_bf[s][:], op=ALU.max)
+            h_codes = pairs.tile([P, COLS], U32, name="h_codes", tag="h_codes", align_bytes=64)
+            h_scales = pairs.tile([P, COLS], U8, name="h_scales", tag="h_scales", align_bytes=64)
+            nc.vector.quantize_mx(out=h_codes[:].bitcast(FP8X4), scales=h_scales[:], in_=h[s][:])
+            return h_codes, h_scales
+
+        def multiply(s, h_codes, h_scales):
+            a, q = steps[s]
             x = []
             for n in range(OUT_TILES):
-                cols = slice(n * P, (n + 1) * P)
-                x.append(psum.tile([P, HALF_ROWS], F32, name="x%d" % n, tag="work"))
-                for target, first, last in ((x[n], True, True), (lin[hf][n], j == 0, j == NODES - 1)):
-                    nc.tensor.matmul_mx(
-                        out=target[:],
-                        lhsT=w2[:, cols].bitcast(FP8X4),
-                        lhsT_scale=w_planes[:, 2, cols],
-                        rhs=h_codes[:].bitcast(FP8X4),
-                        rhs_scale=h_scales[:],
-                        start=first,
-                        stop=last,
-                    )
+                chans = slice(n * P, (n + 1) * P)
+                x.append(banks.tile([P, COLS], F32, name="x%d" % n, tag="bank"))
+                nc.tensor.matmul_mx(
+                    out=x[n][:],
+                    lhsT=w2[:, chans].bitcast(FP8X4),
+                    lhsT_scale=w_planes[:, 2, chans],
+                    rhs=h_codes[:].bitcast(FP8X4),
+                    rhs_scale=h_scales[:],
+                    start=True,
+                    stop=True,
+                )
+            if q == 0:
+                lin[a] = groups.tile([P, C], F32, name="lin", tag="lin")
+            for j in range(J_STEP):
+                cols = slice(j * P, (j + 1) * P)
+                nc.tensor.matmul_mx(
+                    out=lin[a][:],
+                    lhsT=h_codes[:, cols].bitcast(FP8X4),
+                    lhsT_scale=h_scales[:, cols],
+                    rhs=w2[:].bitcast(FP8X4),
+                    rhs_scale=w_planes[:, 2, :],
+                    start=(q == 0 and j == 0),
+                    stop=(q == STEPS_PER_TILE - 1 and j == J_STEP - 1),
+                )
             return x
 
-        def accumulate(s, x):
-            hf, j = steps[s]
-            if j == 0:
-                acc[hf] = sums.tile([P, OUT_TILES, HALF_ROWS], F32, name="acc", tag="acc")
+        def relu(x):
+            r = []
             for n in range(OUT_TILES):
-                if j == 0:
-                    nc.vector.tensor_scalar(
-                        out=acc[hf][:, n, :], in0=x[n][:], scalar1=neg_b2[:, n : n + 1], scalar2=None, op0=ALU.max
+                r.append(relus.tile([P, COLS], F32, name="r%d" % n, tag="r"))
+                nc.scalar.activation(
+                    out=r[n][:], in_=x[n][:], func=ACT.Relu, bias=b2_pos[:, n : n + 1], scale=POS_SLOPE
+                )
+            return r
+
+        def add_up(s, r):
+            a, q = steps[s]
+            if q == 0:
+                pos[a] = groups.tile([P, C], F32, name="pos", tag="pos")
+                for n in range(OUT_TILES):
+                    nc.tensor.matmul(
+                        out=pos[a][:, n * P : (n + 1) * P],
+                        lhsT=b2_squares[:, n, :],
+                        rhs=ident[:],
+                        is_transpose=True,
+                        start=(n == 0),
+                        stop=False,
                     )
-                else:
-                    nc.vector.scalar_tensor_tensor(
-                        out=acc[hf][:, n, :],
-                        in0=x[n][:],
-                        scalar=neg_b2[:, n : n + 1],
-                        in1=acc[hf][:, n, :],
-                        op0=ALU.max,
-                        op1=ALU.add,
+            for j in range(J_STEP):
+                for n in range(OUT_TILES):
+                    nc.tensor.matmul(
+                        out=pos[a][:, n * P : (n + 1) * P],
+                        lhsT=r[n][:, j * P : (j + 1) * P],
+                        rhs=ident[:],
+                        is_transpose=True,
+                        start=False,
+                        stop=(q == STEPS_PER_TILE - 1 and j == J_STEP - 1 and n == OUT_TILES - 1),
                     )
 
-        def finish(hf):
-            for n in range(OUT_TILES):
-                base = sums.tile([P, HALF_ROWS], F32, name="base", tag="base")
-                nc.scalar.activation(
-                    out=base[:], in_=lin[hf][n][:], func=ACT.Identity, bias=b2_x16[:, n : n + 1], scale=NEG_SLOPE
-                )
-                nc.vector.scalar_tensor_tensor(
-                    out=acc[hf][:, n, :],
-                    in0=acc[hf][:, n, :],
-                    scalar=1.0 - NEG_SLOPE,
-                    in1=base[:],
-                    op0=ALU.mult,
-                    op1=ALU.add,
-                )
-            for a in range(HALF_TILES):
-                back = psum.tile([P, C], F32, name="back", tag="work")
-                for n in range(OUT_TILES):
-                    nc.tensor.transpose(back[:, n * P : (n + 1) * P], acc[hf][:, n, a * P : (a + 1) * P], ident[:])
-                result = stage.tile([P, C], F32, name="result", tag="result")
-                nc.scalar.copy(out=result[:], in_=back[:])
-                first_row = hf * HALF_ROWS + a * P
-                nc.sync.dma_start(out=out_rows[first_row : first_row + P, :], in_=result[:])
+        def finish(a):
+            base = stage.tile([P, C], F32, name="base", tag="base")
+            nc.scalar.mul(out=base[:], in_=lin[a][:], mul=NEG_SLOPE)
+            result = stage.tile([P, C], F32, name="result", tag="result")
+            nc.vector.tensor_tensor(out=result[:], in0=pos[a][:], in1=base[:], op=ALU.add)
+            nc.sync.dma_start(out=out_rows[a * P : (a + 1) * P, :], in_=result[:])
 
         for s in range(LEAD):
-            add_pairs(s)
+            round_pairs(s, add_pairs(s))
         for s in range(len(steps)):
-            x = multiply(s)
+            a, q = steps[s]
+            h_codes, h_scales = quantise(s)
+            x = multiply(s, h_codes, h_scales)
             if s + LEAD < len(steps):
-                add_pairs(s + LEAD)
-            accumulate(s, x)
-            if steps[s][1] == NODES - 1:
-                finish(steps[s][0])
+                v = add_pairs(s + LEAD)
+            r = relu(x)
+            if s + LEAD < len(steps):
+                round_pairs(s + LEAD, v)
+            add_up(s, r)
+            if q == 0 and a > 0:
+                finish(a - 1)
+            if a + AHEAD < ROW_TILES:
+                if q == 0:
+                    prepare_codes(a + AHEAD)
+                if q == 1:
+                    prepare_products(a + AHEAD)
+                if q == 2:
+                    prepare_turned(a + AHEAD)
+        finish(ROW_TILES - 1)

@@ -24,7 +24,7 @@ COLS = J_STEP * P
 OUT_TILES = C // P
 NEG_SLOPE = 0.2
 POS_SLOPE = 1.0 - NEG_SLOPE
-SCALAR_COLS = COLS // 2
+SCALAR_COLS = 7 * COLS // 16
 LEAD = 2
 AHEAD = 2
 
@@ -43,13 +43,11 @@ def tile_nonlocalmp_pa_t_kernel(tc, F, W1_words, W1_scales, b1, W2_words, W2_sca
         relus = ctx.enter_context(tc.tile_pool(name="relus", bufs=2 * OUT_TILES))
         banks = ctx.enter_context(tc.psum_pool(name="banks", bufs=4))
         groups = ctx.enter_context(tc.psum_pool(name="groups", bufs=2))
+        ctx.enter_context(tc.manual_schedule())
 
         w_planes = keep.tile([P, 3, C], U8, align_bytes=64)
         nc.vector.memset(w_planes[:].rearrange("p g n -> p (g n)").bitcast(I32), 0)
 
-        f_sb = keep.tile([P, ROW_TILES, C], BF16)
-        f_tiled = f_rows.rearrange("(a p) c -> p a c", p=P)
-        nc.sync.dma_start(out=f_sb[:, 0:AHEAD, :], in_=f_tiled[:, 0:AHEAD, :])
         for quad in range(4):
             nc.sync.dma_start(
                 out=w_planes[32 * quad : 32 * quad + 4, 0:2, :].bitcast(I32),
@@ -64,10 +62,13 @@ def tile_nonlocalmp_pa_t_kernel(tc, F, W1_words, W1_scales, b1, W2_words, W2_sca
             )
         w2 = keep.tile([P, C], U32, align_bytes=64)
         nc.sync.dma_start(out=w2[:].bitcast(I32), in_=W2_words[0].rearrange("p n t -> p (n t)").bitcast(I32))
-        nc.sync.dma_start(out=f_sb[:, AHEAD:ROW_TILES, :], in_=f_tiled[:, AHEAD:ROW_TILES, :])
 
+        f_sb = keep.tile([P, ROW_TILES, C], BF16)
+        f_tiled = f_rows.rearrange("(a p) c -> p a c", p=P)
+        nc.scalar.dma_start(out=f_sb[:, 0:1, :], in_=f_tiled[:, 0:1, :])
         b1_pt = keep.tile([P, PACK], BF16)
         nc.scalar.dma_start(out=b1_pt[:], in_=b1.rearrange("(p t) -> p t", t=PACK))
+        nc.scalar.dma_start(out=f_sb[:, 1:ROW_TILES, :], in_=f_tiled[:, 1:ROW_TILES, :])
         b2_rows = keep.tile([P, P], BF16)
         nc.vector.memset(b2_rows[:], 0.0)
         nc.scalar.dma_start(out=b2_rows[0:OUT_TILES, :], in_=b2.rearrange("(n p) -> n p", p=P))
@@ -89,9 +90,7 @@ def tile_nonlocalmp_pa_t_kernel(tc, F, W1_words, W1_scales, b1, W2_words, W2_sca
             f_ps = banks.tile([P, C], F32, name="f_ps", tag="bank")
             for u in range(2):
                 nc.tensor.transpose(f_ps[:, u * P : (u + 1) * P], f_words[:, u : C // 2 : 2], ident[:])
-            nc.vector.tensor_copy(
-                out=f_grp_words[:, rows, :], in_=f_ps[:, 0 : 2 * P].rearrange("p (u r) -> p r u", u=2)
-            )
+            nc.scalar.copy(out=f_grp_words[:, rows, :], in_=f_ps[:, 0 : 2 * P].rearrange("p (u r) -> p r u", u=2))
             nc.vector.quantize_mx(
                 out=f_codes[:, rows].bitcast(FP8X4),
                 scales=f_scales[:, rows],
@@ -112,11 +111,7 @@ def tile_nonlocalmp_pa_t_kernel(tc, F, W1_words, W1_scales, b1, W2_words, W2_sca
                     stop=True,
                 )
                 sorted_ch[a, g] = stage.tile([P, PACK, P], F32, name="sorted_ch", tag="sorted_ch")
-                by_t = prod[:].rearrange("r (m t) -> r t m", t=PACK)
-                if g == 0:
-                    nc.scalar.copy(out=sorted_ch[a, g][:], in_=by_t)
-                else:
-                    nc.vector.tensor_copy(out=sorted_ch[a, g][:], in_=by_t)
+                nc.scalar.copy(out=sorted_ch[a, g][:], in_=prod[:].rearrange("r (m t) -> r t m", t=PACK))
 
         def prepare_turned(a):
             for g in range(2):
@@ -133,26 +128,24 @@ def tile_nonlocalmp_pa_t_kernel(tc, F, W1_words, W1_scales, b1, W2_words, W2_sca
                         op=ALU.add,
                     )
 
-        for phase in (prepare_codes, prepare_products, prepare_turned):
-            for a in range(AHEAD):
-                phase(a)
-
         b2_square = keep.tile([P, P], F32)
-        nc.vector.tensor_copy(out=b2_square[:], in_=b2_rows[:])
-        b2_ps = banks.tile([P, C], F32, name="b2_ps", tag="bank")
-        nc.tensor.transpose(b2_ps[:, 0:P], b2_square[:], ident[:])
         b2_pos = keep.tile([P, OUT_TILES], F32)
-        nc.vector.tensor_scalar(out=b2_pos[:], in0=b2_ps[:, 0:OUT_TILES], scalar1=POS_SLOPE, scalar2=None, op0=ALU.mult)
         b2_sum = keep.tile([P, OUT_TILES], F32)
-        nc.vector.tensor_scalar(
-            out=b2_sum[:], in0=b2_ps[:, 0:OUT_TILES], scalar1=NODES * NEG_SLOPE, scalar2=None, op0=ALU.mult
-        )
         b2_squares = keep.tile([P, OUT_TILES, P], F32)
-        nc.vector.tensor_copy(out=b2_squares[:], in_=b2_sum[:].unsqueeze(2).to_broadcast([P, OUT_TILES, P]))
+
+        def spread_b2():
+            nc.vector.tensor_copy(out=b2_square[:], in_=b2_rows[:])
+            b2_ps = banks.tile([P, C], F32, name="b2_ps", tag="bank")
+            nc.tensor.transpose(b2_ps[:, 0:P], b2_square[:], ident[:])
+            b2_cols = b2_ps[:, 0:OUT_TILES]
+            nc.vector.tensor_scalar(out=b2_pos[:], in0=b2_cols, scalar1=POS_SLOPE, scalar2=None, op0=ALU.mult)
+            nc.vector.tensor_scalar(out=b2_sum[:], in0=b2_cols, scalar1=NODES * NEG_SLOPE, scalar2=None, op0=ALU.mult)
+            nc.vector.tensor_copy(out=b2_squares[:], in_=b2_sum[:].unsqueeze(2).to_broadcast([P, OUT_TILES, P]))
 
         steps = [(a, q) for a in range(ROW_TILES) for q in range(STEPS_PER_TILE)]
         h, v_bf, w_bf = {}, {}, {}
         lin, pos = {}, {}
+        base = {}
 
         def add_pairs(s):
             a, q = steps[s]
@@ -238,26 +231,35 @@ def tile_nonlocalmp_pa_t_kernel(tc, F, W1_words, W1_scales, b1, W2_words, W2_sca
                         start=(n == 0),
                         stop=False,
                     )
-            for j in range(J_STEP):
-                for n in range(OUT_TILES):
+            for n in range(OUT_TILES):
+                for j in range(J_STEP):
                     nc.tensor.matmul(
                         out=pos[a][:, n * P : (n + 1) * P],
                         lhsT=r[n][:, j * P : (j + 1) * P],
                         rhs=ident[:],
                         is_transpose=True,
                         start=False,
-                        stop=(q == STEPS_PER_TILE - 1 and j == J_STEP - 1 and n == OUT_TILES - 1),
+                        stop=(q == STEPS_PER_TILE - 1 and n == OUT_TILES - 1 and j == J_STEP - 1),
                     )
 
+        def scale_lin(a):
+            base[a] = stage.tile([P, C], F32, name="base", tag="base")
+            nc.scalar.mul(out=base[a][:], in_=lin[a][:], mul=NEG_SLOPE)
+
         def finish(a):
-            base = stage.tile([P, C], F32, name="base", tag="base")
-            nc.scalar.mul(out=base[:], in_=lin[a][:], mul=NEG_SLOPE)
             result = stage.tile([P, C], F32, name="result", tag="result")
-            nc.vector.tensor_tensor(out=result[:], in0=pos[a][:], in1=base[:], op=ALU.add)
+            nc.vector.tensor_tensor(out=result[:], in0=pos[a][:], in1=base[a][:], op=ALU.add)
             nc.sync.dma_start(out=out_rows[a * P : (a + 1) * P, :], in_=result[:])
 
-        for s in range(LEAD):
-            round_pairs(s, add_pairs(s))
+        prepare_codes(0)
+        prepare_products(0)
+        prepare_codes(1)
+        prepare_turned(0)
+        prepare_products(1)
+        round_pairs(0, add_pairs(0))
+        prepare_turned(1)
+        round_pairs(1, add_pairs(1))
+        spread_b2()
         for s in range(len(steps)):
             a, q = steps[s]
             h_codes, h_scales = quantise(s)
@@ -265,11 +267,6 @@ def tile_nonlocalmp_pa_t_kernel(tc, F, W1_words, W1_scales, b1, W2_words, W2_sca
             if s + LEAD < len(steps):
                 v = add_pairs(s + LEAD)
             r = relu(x)
-            if s + LEAD < len(steps):
-                round_pairs(s + LEAD, v)
-            add_up(s, r)
-            if q == 0 and a > 0:
-                finish(a - 1)
             if a + AHEAD < ROW_TILES:
                 if q == 0:
                     prepare_codes(a + AHEAD)
@@ -277,4 +274,11 @@ def tile_nonlocalmp_pa_t_kernel(tc, F, W1_words, W1_scales, b1, W2_words, W2_sca
                     prepare_products(a + AHEAD)
                 if q == 2:
                     prepare_turned(a + AHEAD)
+            if q == STEPS_PER_TILE - 1:
+                scale_lin(a)
+            if s + LEAD < len(steps):
+                round_pairs(s + LEAD, v)
+            add_up(s, r)
+            if q == 0 and a > 0:
+                finish(a - 1)
         finish(ROW_TILES - 1)

@@ -24,8 +24,8 @@ COLS = J_STEP * P
 OUT_TILES = C // P
 NEG_SLOPE = 0.2
 POS_SLOPE = 1.0 - NEG_SLOPE
-SCALAR_COLS = 7 * COLS // 16
-LEAD = 2
+SCALAR_COLS = 13 * COLS // 32
+LEAD = 3
 AHEAD = 2
 
 FLOPS = 2 * ROWS * (2 * C) * C + 2 * SETS * NODES * NODES * C * C
@@ -39,8 +39,8 @@ def tile_nonlocalmp_pa_t_kernel(tc, F, W1_words, W1_scales, b1, W2_words, W2_sca
     with ExitStack() as ctx:
         keep = ctx.enter_context(tc.tile_pool(name="keep", bufs=1))
         stage = ctx.enter_context(tc.tile_pool(name="stage", bufs=4))
-        pairs = ctx.enter_context(tc.tile_pool(name="pairs", bufs=3))
-        relus = ctx.enter_context(tc.tile_pool(name="relus", bufs=2 * OUT_TILES))
+        pairs = ctx.enter_context(tc.tile_pool(name="pairs", bufs=4))
+        relus = ctx.enter_context(tc.tile_pool(name="relus", bufs=3 * OUT_TILES))
         banks = ctx.enter_context(tc.psum_pool(name="banks", bufs=4))
         groups = ctx.enter_context(tc.psum_pool(name="groups", bufs=2))
         ctx.enter_context(tc.manual_schedule())
@@ -83,6 +83,15 @@ def tile_nonlocalmp_pa_t_kernel(tc, F, W1_words, W1_scales, b1, W2_words, W2_sca
         a_t = keep.tile([P, ROW_TILES, P, PACK], F32)
         b_t = keep.tile([P, ROW_TILES, NODES, TILE_SETS, PACK], F32)
         sorted_ch = {}
+        b1_squares = keep.tile([P, PACK, P], F32)
+        b1_rows = keep.tile([P, PACK, P], F32)
+
+        def spread_b1():
+            nc.vector.tensor_copy(out=b1_squares[:], in_=b1_pt[:].unsqueeze(2).to_broadcast([P, PACK, P]))
+            b1_ps = banks.tile([P, C], F32, name="b1_ps", tag="bank")
+            for t in range(PACK):
+                nc.tensor.transpose(b1_ps[:, t * P : (t + 1) * P], b1_squares[:, t, :], ident[:])
+            nc.scalar.copy(out=b1_rows[:].rearrange("r t m -> r (t m)"), in_=b1_ps[:])
 
         def prepare_codes(a):
             rows = slice(a * P, (a + 1) * P)
@@ -117,16 +126,27 @@ def tile_nonlocalmp_pa_t_kernel(tc, F, W1_words, W1_scales, b1, W2_words, W2_sca
             for g in range(2):
                 turned = banks.tile([P, C], F32, name="turned", tag="bank")
                 for t in range(PACK):
-                    nc.tensor.transpose(turned[:, t * P : (t + 1) * P], sorted_ch[a, g][:, t, :], ident[:])
+                    nc.tensor.matmul(
+                        out=turned[:, t * P : (t + 1) * P],
+                        lhsT=sorted_ch[a, g][:, t, :],
+                        rhs=ident[:],
+                        is_transpose=True,
+                        start=(t == 0),
+                        stop=(g == 0 and t == PACK - 1),
+                    )
                 if g == 0:
                     nc.scalar.copy(out=a_t[:, a], in_=turned[:].rearrange("p (t r) -> p r t", t=PACK))
                 else:
-                    nc.vector.tensor_tensor(
-                        out=b_t[:, a],
-                        in0=turned[:].rearrange("p (t b j) -> p j b t", t=PACK, j=NODES),
-                        in1=b1_pt[:].unsqueeze(1).unsqueeze(1).to_broadcast([P, NODES, TILE_SETS, PACK]),
-                        op=ALU.add,
-                    )
+                    for t in range(PACK):
+                        nc.tensor.matmul(
+                            out=turned[:, t * P : (t + 1) * P],
+                            lhsT=b1_rows[:, t, :],
+                            rhs=ident[:],
+                            is_transpose=True,
+                            start=False,
+                            stop=(t == PACK - 1),
+                        )
+                    nc.scalar.copy(out=b_t[:, a], in_=turned[:].rearrange("p (t b j) -> p j b t", t=PACK, j=NODES))
 
         b2_square = keep.tile([P, P], F32)
         b2_pos = keep.tile([P, OUT_TILES], F32)
@@ -143,43 +163,43 @@ def tile_nonlocalmp_pa_t_kernel(tc, F, W1_words, W1_scales, b1, W2_words, W2_sca
             nc.vector.tensor_copy(out=b2_squares[:], in_=b2_sum[:].unsqueeze(2).to_broadcast([P, OUT_TILES, P]))
 
         steps = [(a, q) for a in range(ROW_TILES) for q in range(STEPS_PER_TILE)]
-        h, v_bf, w_bf = {}, {}, {}
+        split = SCALAR_COLS * PACK
+        v, h, v_bf, w_bf, codes, scales, r = {}, {}, {}, {}, {}, {}, {}
         lin, pos = {}, {}
         base = {}
 
         def add_pairs(s):
             a, q = steps[s]
             shape = [P, J_STEP, TILE_SETS, NODES, PACK]
-            v = pairs.tile([P, COLS * PACK], F32, name="v", tag="v")
+            v[s] = pairs.tile([P, COLS * PACK], F32, name="v", tag="v")
             nc.vector.tensor_tensor(
-                out=v[:].rearrange("p (j b i t) -> p j b i t", j=J_STEP, b=TILE_SETS, i=NODES),
+                out=v[s][:].rearrange("p (j b i t) -> p j b i t", j=J_STEP, b=TILE_SETS, i=NODES),
                 in0=a_t[:, a].rearrange("p (b i) t -> p b i t", i=NODES).unsqueeze(1).to_broadcast(shape),
                 in1=b_t[:, a, q * J_STEP : (q + 1) * J_STEP].unsqueeze(3).to_broadcast(shape),
                 op=ALU.add,
             )
-            split = SCALAR_COLS * PACK
+
+        def leaky_by_vector(s):
             h[s] = pairs.tile([P, COLS * PACK], BF16, name="h", tag="h", align_bytes=64)
             nc.vector.scalar_tensor_tensor(
-                out=h[s][:, split:], in0=v[:, split:], scalar=NEG_SLOPE, in1=v[:, split:], op0=ALU.mult, op1=ALU.max
+                out=h[s][:, split:], in0=v[s][:, split:], scalar=NEG_SLOPE, in1=v[s][:, split:], op0=ALU.mult, op1=ALU.max
             )
-            return v
 
-        def round_pairs(s, v):
-            split = SCALAR_COLS * PACK
+        def round_pairs(s):
             v_bf[s] = pairs.tile([P, split], BF16, name="v_bf", tag="v_bf")
             w_bf[s] = pairs.tile([P, split], BF16, name="w_bf", tag="w_bf")
-            nc.scalar.copy(out=v_bf[s][:], in_=v[:, 0:split])
-            nc.scalar.mul(out=w_bf[s][:], in_=v[:, 0:split], mul=NEG_SLOPE)
+            nc.scalar.copy(out=v_bf[s][:], in_=v[s][:, 0:split])
+            nc.scalar.mul(out=w_bf[s][:], in_=v[s][:, 0:split], mul=NEG_SLOPE)
+
+        def leaky_of_roundings(s):
+            nc.vector.tensor_tensor(out=h[s][:, 0:split], in0=v_bf[s][:], in1=w_bf[s][:], op=ALU.max)
 
         def quantise(s):
-            split = SCALAR_COLS * PACK
-            nc.vector.tensor_tensor(out=h[s][:, 0:split], in0=v_bf[s][:], in1=w_bf[s][:], op=ALU.max)
-            h_codes = pairs.tile([P, COLS], U32, name="h_codes", tag="h_codes", align_bytes=64)
-            h_scales = pairs.tile([P, COLS], U8, name="h_scales", tag="h_scales", align_bytes=64)
-            nc.vector.quantize_mx(out=h_codes[:].bitcast(FP8X4), scales=h_scales[:], in_=h[s][:])
-            return h_codes, h_scales
+            codes[s] = pairs.tile([P, COLS], U32, name="codes", tag="codes", align_bytes=64)
+            scales[s] = pairs.tile([P, COLS], U8, name="scales", tag="scales", align_bytes=64)
+            nc.vector.quantize_mx(out=codes[s][:].bitcast(FP8X4), scales=scales[s][:], in_=h[s][:])
 
-        def multiply(s, h_codes, h_scales):
+        def multiply(s):
             a, q = steps[s]
             x = []
             for n in range(OUT_TILES):
@@ -189,8 +209,8 @@ def tile_nonlocalmp_pa_t_kernel(tc, F, W1_words, W1_scales, b1, W2_words, W2_sca
                     out=x[n][:],
                     lhsT=w2[:, chans].bitcast(FP8X4),
                     lhsT_scale=w_planes[:, 2, chans],
-                    rhs=h_codes[:].bitcast(FP8X4),
-                    rhs_scale=h_scales[:],
+                    rhs=codes[s][:].bitcast(FP8X4),
+                    rhs_scale=scales[s][:],
                     start=True,
                     stop=True,
                 )
@@ -200,8 +220,8 @@ def tile_nonlocalmp_pa_t_kernel(tc, F, W1_words, W1_scales, b1, W2_words, W2_sca
                 cols = slice(j * P, (j + 1) * P)
                 nc.tensor.matmul_mx(
                     out=lin[a][:],
-                    lhsT=h_codes[:, cols].bitcast(FP8X4),
-                    lhsT_scale=h_scales[:, cols],
+                    lhsT=codes[s][:, cols].bitcast(FP8X4),
+                    lhsT_scale=scales[s][:, cols],
                     rhs=w2[:].bitcast(FP8X4),
                     rhs_scale=w_planes[:, 2, :],
                     start=(q == 0 and j == 0),
@@ -209,16 +229,15 @@ def tile_nonlocalmp_pa_t_kernel(tc, F, W1_words, W1_scales, b1, W2_words, W2_sca
                 )
             return x
 
-        def relu(x):
-            r = []
+        def relu(s, x):
+            r[s] = []
             for n in range(OUT_TILES):
-                r.append(relus.tile([P, COLS], F32, name="r%d" % n, tag="r"))
+                r[s].append(relus.tile([P, COLS], F32, name="r%d" % n, tag="r"))
                 nc.scalar.activation(
-                    out=r[n][:], in_=x[n][:], func=ACT.Relu, bias=b2_pos[:, n : n + 1], scale=POS_SLOPE
+                    out=r[s][n][:], in_=x[n][:], func=ACT.Relu, bias=b2_pos[:, n : n + 1], scale=POS_SLOPE
                 )
-            return r
 
-        def add_up(s, r):
+        def add_up(s):
             a, q = steps[s]
             if q == 0:
                 pos[a] = groups.tile([P, C], F32, name="pos", tag="pos")
@@ -235,7 +254,7 @@ def tile_nonlocalmp_pa_t_kernel(tc, F, W1_words, W1_scales, b1, W2_words, W2_sca
                 for j in range(J_STEP):
                     nc.tensor.matmul(
                         out=pos[a][:, n * P : (n + 1) * P],
-                        lhsT=r[n][:, j * P : (j + 1) * P],
+                        lhsT=r[s][n][:, j * P : (j + 1) * P],
                         rhs=ident[:],
                         is_transpose=True,
                         start=False,
@@ -252,33 +271,49 @@ def tile_nonlocalmp_pa_t_kernel(tc, F, W1_words, W1_scales, b1, W2_words, W2_sca
             nc.sync.dma_start(out=out_rows[a * P : (a + 1) * P, :], in_=result[:])
 
         prepare_codes(0)
+        spread_b1()
         prepare_products(0)
         prepare_codes(1)
         prepare_turned(0)
         prepare_products(1)
-        round_pairs(0, add_pairs(0))
+        add_pairs(0)
+        leaky_by_vector(0)
+        round_pairs(0)
         prepare_turned(1)
-        round_pairs(1, add_pairs(1))
+        add_pairs(1)
+        leaky_by_vector(1)
+        round_pairs(1)
         spread_b2()
-        for s in range(len(steps)):
-            a, q = steps[s]
-            h_codes, h_scales = quantise(s)
-            x = multiply(s, h_codes, h_scales)
+        leaky_of_roundings(0)
+        add_pairs(2)
+        quantise(0)
+        leaky_by_vector(2)
+        round_pairs(2)
+
+        for s in range(len(steps) + 1):
+            a, q = divmod(s, STEPS_PER_TILE)
+            if s + 1 < len(steps):
+                leaky_of_roundings(s + 1)
             if s + LEAD < len(steps):
-                v = add_pairs(s + LEAD)
-            r = relu(x)
-            if a + AHEAD < ROW_TILES:
-                if q == 0:
-                    prepare_codes(a + AHEAD)
-                if q == 1:
-                    prepare_products(a + AHEAD)
-                if q == 2:
-                    prepare_turned(a + AHEAD)
-            if q == STEPS_PER_TILE - 1:
+                add_pairs(s + LEAD)
+            if s + 1 < len(steps):
+                quantise(s + 1)
+            if s + LEAD < len(steps):
+                leaky_by_vector(s + LEAD)
+            if s < len(steps):
+                relu(s, multiply(s))
+            if a + AHEAD < ROW_TILES and q == 0:
+                prepare_codes(a + AHEAD)
+            if a + AHEAD < ROW_TILES and q == 1:
+                prepare_products(a + AHEAD)
+            if a + AHEAD < ROW_TILES and q == 2:
+                prepare_turned(a + AHEAD)
+            if s > 0:
+                add_up(s - 1)
+            if s < len(steps) and q == STEPS_PER_TILE - 1:
                 scale_lin(a)
             if s + LEAD < len(steps):
-                round_pairs(s + LEAD, v)
-            add_up(s, r)
-            if q == 0 and a > 0:
+                round_pairs(s + LEAD)
+            if q == 1 and a > 0:
                 finish(a - 1)
         finish(ROW_TILES - 1)

@@ -24,7 +24,8 @@ COLS = J_STEP * P
 OUT_TILES = C // P
 NEG_SLOPE = 0.2
 POS_SLOPE = 1.0 - NEG_SLOPE
-SCALAR_COLS = 13 * COLS // 32
+SHARE = 13
+WIDTHS = {ROW_TILES - 1: [2] * 8}
 LEAD = 3
 AHEAD = 2
 
@@ -76,6 +77,10 @@ def tile_nonlocalmp_pa_t_kernel(tc, F, W1_words, W1_scales, b1, W2_words, W2_sca
         ident = keep.tile([P, P], F32)
         make_identity(nc, ident[:])
 
+        warm = keep.tile([P, 2], F32)
+        nc.vector.memset(warm[:], 0.0)
+        nc.scalar.activation(out=warm[:, 1:2], in_=warm[:, 0:1], func=ACT.Relu)
+
         f_grp = keep.tile([P, ROWS, PACK], BF16, align_bytes=64)
         f_grp_words = f_grp[:].rearrange("p r t -> p (r t)").bitcast(F32).rearrange("p (r u) -> p r u", u=2)
         f_codes = keep.tile([P, ROWS], U32, align_bytes=64)
@@ -100,13 +105,16 @@ def tile_nonlocalmp_pa_t_kernel(tc, F, W1_words, W1_scales, b1, W2_words, W2_sca
             for u in range(2):
                 nc.tensor.transpose(f_ps[:, u * P : (u + 1) * P], f_words[:, u : C // 2 : 2], ident[:])
             nc.scalar.copy(out=f_grp_words[:, rows, :], in_=f_ps[:, 0 : 2 * P].rearrange("p (u r) -> p r u", u=2))
+
+        def quantise_rows(a):
+            rows = slice(a * P, (a + 1) * P)
             nc.vector.quantize_mx(
                 out=f_codes[:, rows].bitcast(FP8X4),
                 scales=f_scales[:, rows],
                 in_=f_grp[:, rows, :].rearrange("p r t -> p (r t)"),
             )
 
-        def prepare_products(a):
+        def prepare_products(a, shared=False):
             rows = slice(a * P, (a + 1) * P)
             for g in range(2):
                 prod = banks.tile([P, C], F32, name="prod", tag="bank")
@@ -120,9 +128,12 @@ def tile_nonlocalmp_pa_t_kernel(tc, F, W1_words, W1_scales, b1, W2_words, W2_sca
                     stop=True,
                 )
                 sorted_ch[a, g] = stage.tile([P, PACK, P], F32, name="sorted_ch", tag="sorted_ch")
-                nc.scalar.copy(out=sorted_ch[a, g][:], in_=prod[:].rearrange("r (m t) -> r t m", t=PACK))
+                if shared and g == 1:
+                    nc.vector.tensor_copy(out=sorted_ch[a, g][:], in_=prod[:].rearrange("r (m t) -> r t m", t=PACK))
+                else:
+                    nc.scalar.copy(out=sorted_ch[a, g][:], in_=prod[:].rearrange("r (m t) -> r t m", t=PACK))
 
-        def prepare_turned(a):
+        def prepare_turned(a, shared=False):
             for g in range(2):
                 turned = banks.tile([P, C], F32, name="turned", tag="bank")
                 for t in range(PACK):
@@ -134,7 +145,9 @@ def tile_nonlocalmp_pa_t_kernel(tc, F, W1_words, W1_scales, b1, W2_words, W2_sca
                         start=(t == 0),
                         stop=(g == 0 and t == PACK - 1),
                     )
-                if g == 0:
+                if g == 0 and shared:
+                    nc.vector.tensor_copy(out=a_t[:, a], in_=turned[:].rearrange("p (t r) -> p r t", t=PACK))
+                elif g == 0:
                     nc.scalar.copy(out=a_t[:, a], in_=turned[:].rearrange("p (t r) -> p r t", t=PACK))
                 else:
                     for t in range(PACK):
@@ -162,61 +175,82 @@ def tile_nonlocalmp_pa_t_kernel(tc, F, W1_words, W1_scales, b1, W2_words, W2_sca
             nc.vector.tensor_scalar(out=b2_sum[:], in0=b2_cols, scalar1=NODES * NEG_SLOPE, scalar2=None, op0=ALU.mult)
             nc.vector.tensor_copy(out=b2_squares[:], in_=b2_sum[:].unsqueeze(2).to_broadcast([P, OUT_TILES, P]))
 
-        steps = [(a, q) for a in range(ROW_TILES) for q in range(STEPS_PER_TILE)]
-        split = SCALAR_COLS * PACK
+        steps = []
+        for a in range(ROW_TILES):
+            j0 = 0
+            for width in WIDTHS.get(a, [J_STEP] * STEPS_PER_TILE):
+                steps.append((a, j0, width))
+                j0 += width
+
+        def split_of(s):
+            return SHARE * steps[s][2] * P // 32 * PACK
+
+        def width_of(s):
+            return steps[s][2] * P * PACK
         v, h, v_bf, w_bf, codes, scales, r = {}, {}, {}, {}, {}, {}, {}
         lin, pos = {}, {}
         base = {}
 
         def add_pairs(s):
-            a, q = steps[s]
-            shape = [P, J_STEP, TILE_SETS, NODES, PACK]
+            a, j0, nj = steps[s]
+            shape = [P, nj, TILE_SETS, NODES, PACK]
             v[s] = pairs.tile([P, COLS * PACK], F32, name="v", tag="v")
             nc.vector.tensor_tensor(
-                out=v[s][:].rearrange("p (j b i t) -> p j b i t", j=J_STEP, b=TILE_SETS, i=NODES),
+                out=v[s][:, 0 : width_of(s)].rearrange("p (j b i t) -> p j b i t", j=nj, b=TILE_SETS, i=NODES),
                 in0=a_t[:, a].rearrange("p (b i) t -> p b i t", i=NODES).unsqueeze(1).to_broadcast(shape),
-                in1=b_t[:, a, q * J_STEP : (q + 1) * J_STEP].unsqueeze(3).to_broadcast(shape),
+                in1=b_t[:, a, j0 : j0 + nj].unsqueeze(3).to_broadcast(shape),
                 op=ALU.add,
             )
 
         def leaky_by_vector(s):
             h[s] = pairs.tile([P, COLS * PACK], BF16, name="h", tag="h", align_bytes=64)
             nc.vector.scalar_tensor_tensor(
-                out=h[s][:, split:], in0=v[s][:, split:], scalar=NEG_SLOPE, in1=v[s][:, split:], op0=ALU.mult, op1=ALU.max
+                out=h[s][:, split_of(s) : width_of(s)],
+                in0=v[s][:, split_of(s) : width_of(s)],
+                scalar=NEG_SLOPE,
+                in1=v[s][:, split_of(s) : width_of(s)],
+                op0=ALU.mult,
+                op1=ALU.max,
             )
 
         def round_pairs(s):
+            split = split_of(s)
             v_bf[s] = pairs.tile([P, split], BF16, name="v_bf", tag="v_bf")
             w_bf[s] = pairs.tile([P, split], BF16, name="w_bf", tag="w_bf")
             nc.scalar.copy(out=v_bf[s][:], in_=v[s][:, 0:split])
             nc.scalar.mul(out=w_bf[s][:], in_=v[s][:, 0:split], mul=NEG_SLOPE)
 
         def leaky_of_roundings(s):
+            split = split_of(s)
             nc.vector.tensor_tensor(out=h[s][:, 0:split], in0=v_bf[s][:], in1=w_bf[s][:], op=ALU.max)
 
         def quantise(s):
             codes[s] = pairs.tile([P, COLS], U32, name="codes", tag="codes", align_bytes=64)
             scales[s] = pairs.tile([P, COLS], U8, name="scales", tag="scales", align_bytes=64)
-            nc.vector.quantize_mx(out=codes[s][:].bitcast(FP8X4), scales=scales[s][:], in_=h[s][:])
+            cols = steps[s][2] * P
+            nc.vector.quantize_mx(
+                out=codes[s][:, 0:cols].bitcast(FP8X4), scales=scales[s][:, 0:cols], in_=h[s][:, 0 : width_of(s)]
+            )
 
         def multiply(s):
-            a, q = steps[s]
+            a, j0, nj = steps[s]
+            cols = nj * P
             x = []
             for n in range(OUT_TILES):
                 chans = slice(n * P, (n + 1) * P)
                 x.append(banks.tile([P, COLS], F32, name="x%d" % n, tag="bank"))
                 nc.tensor.matmul_mx(
-                    out=x[n][:],
+                    out=x[n][:, 0:cols],
                     lhsT=w2[:, chans].bitcast(FP8X4),
                     lhsT_scale=w_planes[:, 2, chans],
-                    rhs=codes[s][:].bitcast(FP8X4),
-                    rhs_scale=scales[s][:],
+                    rhs=codes[s][:, 0:cols].bitcast(FP8X4),
+                    rhs_scale=scales[s][:, 0:cols],
                     start=True,
                     stop=True,
                 )
-            if q == 0:
+            if j0 == 0:
                 lin[a] = groups.tile([P, C], F32, name="lin", tag="lin")
-            for j in range(J_STEP):
+            for j in range(nj):
                 cols = slice(j * P, (j + 1) * P)
                 nc.tensor.matmul_mx(
                     out=lin[a][:],
@@ -224,8 +258,8 @@ def tile_nonlocalmp_pa_t_kernel(tc, F, W1_words, W1_scales, b1, W2_words, W2_sca
                     lhsT_scale=scales[s][:, cols],
                     rhs=w2[:].bitcast(FP8X4),
                     rhs_scale=w_planes[:, 2, :],
-                    start=(q == 0 and j == 0),
-                    stop=(q == STEPS_PER_TILE - 1 and j == J_STEP - 1),
+                    start=(j0 + j == 0),
+                    stop=(j0 + j == NODES - 1),
                 )
             return x
 
@@ -233,13 +267,14 @@ def tile_nonlocalmp_pa_t_kernel(tc, F, W1_words, W1_scales, b1, W2_words, W2_sca
             r[s] = []
             for n in range(OUT_TILES):
                 r[s].append(relus.tile([P, COLS], F32, name="r%d" % n, tag="r"))
+                cols = steps[s][2] * P
                 nc.scalar.activation(
-                    out=r[s][n][:], in_=x[n][:], func=ACT.Relu, bias=b2_pos[:, n : n + 1], scale=POS_SLOPE
+                    out=r[s][n][:, 0:cols], in_=x[n][:, 0:cols], func=ACT.Relu, bias=b2_pos[:, n : n + 1], scale=POS_SLOPE
                 )
 
         def add_up(s):
-            a, q = steps[s]
-            if q == 0:
+            a, j0, nj = steps[s]
+            if j0 == 0:
                 pos[a] = groups.tile([P, C], F32, name="pos", tag="pos")
                 for n in range(OUT_TILES):
                     nc.tensor.matmul(
@@ -251,14 +286,14 @@ def tile_nonlocalmp_pa_t_kernel(tc, F, W1_words, W1_scales, b1, W2_words, W2_sca
                         stop=False,
                     )
             for n in range(OUT_TILES):
-                for j in range(J_STEP):
+                for j in range(nj):
                     nc.tensor.matmul(
                         out=pos[a][:, n * P : (n + 1) * P],
                         lhsT=r[s][n][:, j * P : (j + 1) * P],
                         rhs=ident[:],
                         is_transpose=True,
                         start=False,
-                        stop=(q == STEPS_PER_TILE - 1 and n == OUT_TILES - 1 and j == J_STEP - 1),
+                        stop=(j0 + nj == NODES and n == OUT_TILES - 1 and j == nj - 1),
                     )
 
         def scale_lin(a):
@@ -271,12 +306,14 @@ def tile_nonlocalmp_pa_t_kernel(tc, F, W1_words, W1_scales, b1, W2_words, W2_sca
             nc.sync.dma_start(out=out_rows[a * P : (a + 1) * P, :], in_=result[:])
 
         prepare_codes(0)
+        quantise_rows(0)
         spread_b1()
-        prepare_products(0)
+        prepare_products(0, shared=True)
+        prepare_turned(0, shared=True)
         prepare_codes(1)
-        prepare_turned(0)
-        prepare_products(1)
         add_pairs(0)
+        quantise_rows(1)
+        prepare_products(1)
         leaky_by_vector(0)
         round_pairs(0)
         prepare_turned(1)
@@ -291,7 +328,8 @@ def tile_nonlocalmp_pa_t_kernel(tc, F, W1_words, W1_scales, b1, W2_words, W2_sca
         round_pairs(2)
 
         for s in range(len(steps) + 1):
-            a, q = divmod(s, STEPS_PER_TILE)
+            a, j0, nj = steps[s] if s < len(steps) else (ROW_TILES, 0, 0)
+            q = j0 // J_STEP if nj == J_STEP else -1
             if s + 1 < len(steps):
                 leaky_of_roundings(s + 1)
             if s + LEAD < len(steps):
@@ -304,16 +342,17 @@ def tile_nonlocalmp_pa_t_kernel(tc, F, W1_words, W1_scales, b1, W2_words, W2_sca
                 relu(s, multiply(s))
             if a + AHEAD < ROW_TILES and q == 0:
                 prepare_codes(a + AHEAD)
+                quantise_rows(a + AHEAD)
             if a + AHEAD < ROW_TILES and q == 1:
                 prepare_products(a + AHEAD)
             if a + AHEAD < ROW_TILES and q == 2:
                 prepare_turned(a + AHEAD)
             if s > 0:
                 add_up(s - 1)
-            if s < len(steps) and q == STEPS_PER_TILE - 1:
+            if s < len(steps) and j0 + nj == NODES:
                 scale_lin(a)
             if s + LEAD < len(steps):
                 round_pairs(s + LEAD)
-            if q == 1 and a > 0:
-                finish(a - 1)
+            if s > 0 and s - 1 < len(steps) and steps[s - 1][1] == 0 and steps[s - 1][0] > 0:
+                finish(steps[s - 1][0] - 1)
         finish(ROW_TILES - 1)

@@ -24,7 +24,7 @@ COLS = J_STEP * P
 OUT_TILES = C // P
 NEG_SLOPE = 0.2
 POS_SLOPE = 1.0 - NEG_SLOPE
-SHARE = 13
+SHARE = 12
 WIDTHS = {ROW_TILES - 1: [2] * 8}
 LEAD = 3
 AHEAD = 2

@@ -69,10 +69,11 @@ def tile_nonlocalmp_pa_t_kernel(tc, F, W1_words, W1_scales, b1, W2_words, W2_sca
         nc.scalar.dma_start(out=f_sb[:, 0:1, :], in_=f_tiled[:, 0:1, :])
         b1_pt = keep.tile([P, PACK], BF16)
         nc.scalar.dma_start(out=b1_pt[:], in_=b1.rearrange("(p t) -> p t", t=PACK))
-        nc.scalar.dma_start(out=f_sb[:, 1:ROW_TILES, :], in_=f_tiled[:, 1:ROW_TILES, :])
         b2_rows = keep.tile([P, P], BF16)
         nc.vector.memset(b2_rows[:], 0.0)
         nc.scalar.dma_start(out=b2_rows[0:OUT_TILES, :], in_=b2.rearrange("(n p) -> n p", p=P))
+        nc.sync.dma_start(out=f_sb[:, 1:2, :], in_=f_tiled[:, 1:2, :])
+        nc.sync.dma_start(out=f_sb[:, 2:ROW_TILES, :], in_=f_tiled[:, 2:ROW_TILES, :])
 
         ident = keep.tile([P, P], F32)
         make_identity(nc, ident[:])

@@ -49,13 +49,18 @@ def tile_nonlocalmp_pa_t_kernel(tc, F, W1_words, W1_scales, b1, W2_words, W2_sca
         w_planes = keep.tile([P, 3, C], U8, align_bytes=64)
         nc.vector.memset(w_planes[:].rearrange("p g n -> p (g n)").bitcast(I32), 0)
 
+        f_sb = keep.tile([P, ROW_TILES, C], BF16)
+        f_tiled = f_rows.rearrange("(a p) c -> p a c", p=P)
+        nc.sync.dma_start(out=f_sb[:, 0:1, :], in_=f_tiled[:, 0:1, :])
+        b1_pt = keep.tile([P, PACK], BF16)
+        nc.sync.dma_start(out=b1_pt[:], in_=b1.rearrange("(p t) -> p t", t=PACK))
+        w1 = keep.tile([P, 2, C], U32, align_bytes=64)
+        nc.sync.dma_start(out=w1[:].bitcast(I32), in_=W1_words.rearrange("g p n t -> p g (n t)").bitcast(I32))
         for quad in range(4):
             nc.sync.dma_start(
                 out=w_planes[32 * quad : 32 * quad + 4, 0:2, :].bitcast(I32),
                 in_=W1_scales[:, 4 * quad : 4 * quad + 4, :].rearrange("g r n -> r g n").bitcast(I32),
             )
-        w1 = keep.tile([P, 2, C], U32, align_bytes=64)
-        nc.sync.dma_start(out=w1[:].bitcast(I32), in_=W1_words.rearrange("g p n t -> p g (n t)").bitcast(I32))
         for quad in range(4):
             nc.sync.dma_start(
                 out=w_planes[32 * quad : 32 * quad + 4, 2, :].bitcast(I32),
@@ -63,17 +68,11 @@ def tile_nonlocalmp_pa_t_kernel(tc, F, W1_words, W1_scales, b1, W2_words, W2_sca
             )
         w2 = keep.tile([P, C], U32, align_bytes=64)
         nc.sync.dma_start(out=w2[:].bitcast(I32), in_=W2_words[0].rearrange("p n t -> p (n t)").bitcast(I32))
-
-        f_sb = keep.tile([P, ROW_TILES, C], BF16)
-        f_tiled = f_rows.rearrange("(a p) c -> p a c", p=P)
-        nc.scalar.dma_start(out=f_sb[:, 0:1, :], in_=f_tiled[:, 0:1, :])
-        b1_pt = keep.tile([P, PACK], BF16)
-        nc.scalar.dma_start(out=b1_pt[:], in_=b1.rearrange("(p t) -> p t", t=PACK))
-        b2_rows = keep.tile([P, P], BF16)
-        nc.vector.memset(b2_rows[:], 0.0)
-        nc.scalar.dma_start(out=b2_rows[0:OUT_TILES, :], in_=b2.rearrange("(n p) -> n p", p=P))
         nc.sync.dma_start(out=f_sb[:, 1:2, :], in_=f_tiled[:, 1:2, :])
         nc.sync.dma_start(out=f_sb[:, 2:ROW_TILES, :], in_=f_tiled[:, 2:ROW_TILES, :])
+        b2_rows = keep.tile([P, P], BF16)
+        nc.vector.memset(b2_rows[:], 0.0)
+        nc.sync.dma_start(out=b2_rows[0:OUT_TILES, :], in_=b2.rearrange("(n p) -> n p", p=P))
 
         ident = keep.tile([P, P], F32)
         make_identity(nc, ident[:])
@@ -97,7 +96,7 @@ def tile_nonlocalmp_pa_t_kernel(tc, F, W1_words, W1_scales, b1, W2_words, W2_sca
             b1_ps = banks.tile([P, C], F32, name="b1_ps", tag="bank")
             for t in range(PACK):
                 nc.tensor.transpose(b1_ps[:, t * P : (t + 1) * P], b1_squares[:, t, :], ident[:])
-            nc.scalar.copy(out=b1_rows[:].rearrange("r t m -> r (t m)"), in_=b1_ps[:])
+            nc.vector.tensor_copy(out=b1_rows[:].rearrange("r t m -> r (t m)"), in_=b1_ps[:])
 
         def prepare_codes(a):
             rows = slice(a * P, (a + 1) * P)
@@ -135,32 +134,45 @@ def tile_nonlocalmp_pa_t_kernel(tc, F, W1_words, W1_scales, b1, W2_words, W2_sca
                     nc.scalar.copy(out=sorted_ch[a, g][:], in_=prod[:].rearrange("r (m t) -> r t m", t=PACK))
 
         def prepare_turned(a, shared=False):
-            for g in range(2):
-                turned = banks.tile([P, C], F32, name="turned", tag="bank")
-                for t in range(PACK):
-                    nc.tensor.matmul(
-                        out=turned[:, t * P : (t + 1) * P],
-                        lhsT=sorted_ch[a, g][:, t, :],
-                        rhs=ident[:],
-                        is_transpose=True,
-                        start=(t == 0),
-                        stop=(g == 0 and t == PACK - 1),
-                    )
-                if g == 0 and shared:
-                    nc.vector.tensor_copy(out=a_t[:, a], in_=turned[:].rearrange("p (t r) -> p r t", t=PACK))
-                elif g == 0:
-                    nc.scalar.copy(out=a_t[:, a], in_=turned[:].rearrange("p (t r) -> p r t", t=PACK))
-                else:
-                    for t in range(PACK):
-                        nc.tensor.matmul(
-                            out=turned[:, t * P : (t + 1) * P],
-                            lhsT=b1_rows[:, t, :],
-                            rhs=ident[:],
-                            is_transpose=True,
-                            start=False,
-                            stop=(t == PACK - 1),
-                        )
-                    nc.scalar.copy(out=b_t[:, a], in_=turned[:].rearrange("p (t b j) -> p j b t", t=PACK, j=NODES))
+            turned_b = banks.tile([P, C], F32, name="turned_b", tag="bank")
+            for t in range(PACK):
+                nc.tensor.matmul(
+                    out=turned_b[:, t * P : (t + 1) * P],
+                    lhsT=b1_rows[:, t, :],
+                    rhs=ident[:],
+                    is_transpose=True,
+                    start=(t == 0),
+                    stop=False,
+                )
+            turned_a = banks.tile([P, C], F32, name="turned_a", tag="bank")
+            for t in range(PACK):
+                nc.tensor.matmul(
+                    out=turned_a[:, t * P : (t + 1) * P],
+                    lhsT=sorted_ch[a, 0][:, t, :],
+                    rhs=ident[:],
+                    is_transpose=True,
+                    start=(t == 0),
+                    stop=(t == PACK - 1),
+                )
+            if shared:
+                nc.vector.tensor_copy(out=a_t[:, a], in_=turned_a[:].rearrange("p (t r) -> p r t", t=PACK))
+            else:
+                nc.scalar.copy(out=a_t[:, a], in_=turned_a[:].rearrange("p (t r) -> p r t", t=PACK))
+            for t in range(PACK):
+                nc.tensor.matmul(
+                    out=turned_b[:, t * P : (t + 1) * P],
+                    lhsT=sorted_ch[a, 1][:, t, :],
+                    rhs=ident[:],
+                    is_transpose=True,
+                    start=False,
+                    stop=(t == PACK - 1),
+                )
+            by_j = turned_b[:].rearrange("p (t b j) -> p j b t", t=PACK, j=NODES)
+            if shared:
+                nc.scalar.copy(out=b_t[:, a, 0:J_STEP], in_=by_j[:, 0:J_STEP])
+                nc.scalar.copy(out=b_t[:, a, J_STEP:NODES], in_=by_j[:, J_STEP:NODES])
+            else:
+                nc.scalar.copy(out=b_t[:, a], in_=by_j)
 
         b2_square = keep.tile([P, P], F32)
         b2_pos = keep.tile([P, OUT_TILES], F32)

@@ -41,6 +41,7 @@ def tile_nonlocalmp_pa_t_kernel(tc, F, W1_words, W1_scales, b1, W2_words, W2_sca
         keep = ctx.enter_context(tc.tile_pool(name="keep", bufs=1))
         stage = ctx.enter_context(tc.tile_pool(name="stage", bufs=4))
         pairs = ctx.enter_context(tc.tile_pool(name="pairs", bufs=4))
+        late = ctx.enter_context(tc.tile_pool(name="late", bufs=ROW_TILES))
         relus = ctx.enter_context(tc.tile_pool(name="relus", bufs=3 * OUT_TILES))
         banks = ctx.enter_context(tc.psum_pool(name="banks", bufs=4))
         groups = ctx.enter_context(tc.psum_pool(name="groups", bufs=2))
@@ -54,6 +55,9 @@ def tile_nonlocalmp_pa_t_kernel(tc, F, W1_words, W1_scales, b1, W2_words, W2_sca
         nc.sync.dma_start(out=f_sb[:, 0:1, :], in_=f_tiled[:, 0:1, :])
         b1_pt = keep.tile([P, PACK], BF16)
         nc.sync.dma_start(out=b1_pt[:], in_=b1.rearrange("(p t) -> p t", t=PACK))
+        b2_rows = keep.tile([P, P], BF16)
+        nc.vector.memset(b2_rows[:], 0.0)
+        nc.sync.dma_start(out=b2_rows[0:OUT_TILES, :], in_=b2.rearrange("(n p) -> n p", p=P))
         w1 = keep.tile([P, 2, C], U32, align_bytes=64)
         nc.sync.dma_start(out=w1[:].bitcast(I32), in_=W1_words.rearrange("g p n t -> p g (n t)").bitcast(I32))
         for quad in range(4):
@@ -70,9 +74,6 @@ def tile_nonlocalmp_pa_t_kernel(tc, F, W1_words, W1_scales, b1, W2_words, W2_sca
         nc.sync.dma_start(out=w2[:].bitcast(I32), in_=W2_words[0].rearrange("p n t -> p (n t)").bitcast(I32))
         nc.sync.dma_start(out=f_sb[:, 1:2, :], in_=f_tiled[:, 1:2, :])
         nc.sync.dma_start(out=f_sb[:, 2:ROW_TILES, :], in_=f_tiled[:, 2:ROW_TILES, :])
-        b2_rows = keep.tile([P, P], BF16)
-        nc.vector.memset(b2_rows[:], 0.0)
-        nc.sync.dma_start(out=b2_rows[0:OUT_TILES, :], in_=b2.rearrange("(n p) -> n p", p=P))
 
         ident = keep.tile([P, P], F32)
         make_identity(nc, ident[:])
@@ -180,13 +181,13 @@ def tile_nonlocalmp_pa_t_kernel(tc, F, W1_words, W1_scales, b1, W2_words, W2_sca
         b2_squares = keep.tile([P, OUT_TILES, P], F32)
 
         def spread_b2():
-            nc.vector.tensor_copy(out=b2_square[:], in_=b2_rows[:])
+            nc.scalar.copy(out=b2_square[:], in_=b2_rows[:])
             b2_ps = banks.tile([P, C], F32, name="b2_ps", tag="bank")
             nc.tensor.transpose(b2_ps[:, 0:P], b2_square[:], ident[:])
             b2_cols = b2_ps[:, 0:OUT_TILES]
-            nc.vector.tensor_scalar(out=b2_pos[:], in0=b2_cols, scalar1=POS_SLOPE, scalar2=None, op0=ALU.mult)
-            nc.vector.tensor_scalar(out=b2_sum[:], in0=b2_cols, scalar1=NODES * NEG_SLOPE, scalar2=None, op0=ALU.mult)
-            nc.vector.tensor_copy(out=b2_squares[:], in_=b2_sum[:].unsqueeze(2).to_broadcast([P, OUT_TILES, P]))
+            nc.scalar.mul(out=b2_pos[:], in_=b2_cols, mul=POS_SLOPE)
+            nc.scalar.mul(out=b2_sum[:], in_=b2_cols, mul=NODES * NEG_SLOPE)
+            nc.scalar.copy(out=b2_squares[:], in_=b2_sum[:].unsqueeze(2).to_broadcast([P, OUT_TILES, P]))
 
         steps = []
         for a in range(ROW_TILES):
@@ -310,8 +311,19 @@ def tile_nonlocalmp_pa_t_kernel(tc, F, W1_words, W1_scales, b1, W2_words, W2_sca
                     )
 
         def scale_lin(a):
-            base[a] = stage.tile([P, C], F32, name="base", tag="base")
+            base[a] = late.tile([P, C], F32, name="base", tag="base")
             nc.scalar.mul(out=base[a][:], in_=lin[a][:], mul=NEG_SLOPE)
+
+        pos_sb = {}
+
+        def take_pos(a):
+            pos_sb[a] = late.tile([P, C], F32, name="pos_sb", tag="pos_sb")
+            nc.scalar.copy(out=pos_sb[a][:], in_=pos[a][:])
+
+        def finish_late(a):
+            result = stage.tile([P, C], F32, name="result", tag="result")
+            nc.vector.tensor_tensor(out=result[:], in0=pos_sb[a][:], in1=base[a][:], op=ALU.add)
+            nc.sync.dma_start(out=out_rows[a * P : (a + 1) * P, :], in_=result[:])
 
         def finish(a):
             result = stage.tile([P, C], F32, name="result", tag="result")
@@ -321,6 +333,7 @@ def tile_nonlocalmp_pa_t_kernel(tc, F, W1_words, W1_scales, b1, W2_words, W2_sca
         prepare_codes(0)
         quantise_rows(0)
         spread_b1()
+        spread_b2()
         prepare_products(0, shared=True)
         prepare_turned(0, shared=True)
         prepare_codes(1)
@@ -333,7 +346,6 @@ def tile_nonlocalmp_pa_t_kernel(tc, F, W1_words, W1_scales, b1, W2_words, W2_sca
         add_pairs(1)
         leaky_by_vector(1)
         round_pairs(1)
-        spread_b2()
         leaky_of_roundings(0)
         add_pairs(2)
         quantise(0)
@@ -367,5 +379,7 @@ def tile_nonlocalmp_pa_t_kernel(tc, F, W1_words, W1_scales, b1, W2_words, W2_sca
             if s + LEAD < len(steps):
                 round_pairs(s + LEAD)
             if s > 0 and s - 1 < len(steps) and steps[s - 1][1] == 0 and steps[s - 1][0] > 0:
-                finish(steps[s - 1][0] - 1)
+                take_pos(steps[s - 1][0] - 1)
+        for a in range(ROW_TILES - 1):
+            finish_late(a)
         finish(ROW_TILES - 1)

@@ -24,7 +24,7 @@ COLS = J_STEP * P
 OUT_TILES = C // P
 NEG_SLOPE = 0.2
 POS_SLOPE = 1.0 - NEG_SLOPE
-SHARE = 12
+SHARE = 11
 WIDTHS = {ROW_TILES - 1: [2] * 8}
 LEAD = 3
 AHEAD = 2

@@ -26,6 +26,7 @@ NEG_SLOPE = 0.2
 POS_SLOPE = 1.0 - NEG_SLOPE
 SHARE = 11
 WIDTHS = {ROW_TILES - 1: [2] * 8}
+WARM_UP = 3
 LEAD = 3
 AHEAD = 2
 
@@ -46,6 +47,12 @@ def tile_nonlocalmp_pa_t_kernel(tc, F, W1_words, W1_scales, b1, W2_words, W2_sca
         banks = ctx.enter_context(tc.psum_pool(name="banks", bufs=4))
         groups = ctx.enter_context(tc.psum_pool(name="groups", bufs=2))
         ctx.enter_context(tc.manual_schedule())
+
+        zeros = keep.tile([P, C], BF16)
+        nc.gpsimd.memset(zeros[:], 0.0)
+        spare = banks.tile([P, C], F32, name="spare", tag="bank")
+        for k in range(WARM_UP):
+            nc.tensor.matmul(out=spare[:], lhsT=zeros[:, 0:P], rhs=zeros[:], start=True, stop=True)
 
         w_planes = keep.tile([P, 3, C], U8, align_bytes=64)
         nc.vector.memset(w_planes[:].rearrange("p g n -> p (g n)").bitcast(I32), 0)

@@ -24,7 +24,7 @@ COLS = J_STEP * P
 OUT_TILES = C // P
 NEG_SLOPE = 0.2
 POS_SLOPE = 1.0 - NEG_SLOPE
-SHARE = 11
+SHARE = 21
 WIDTHS = {ROW_TILES - 1: [2] * 8}
 WARM_UP = 3
 LEAD = 3
@@ -42,10 +42,12 @@ def tile_nonlocalmp_pa_t_kernel(tc, F, W1_words, W1_scales, b1, W2_words, W2_sca
         keep = ctx.enter_context(tc.tile_pool(name="keep", bufs=1))
         stage = ctx.enter_context(tc.tile_pool(name="stage", bufs=4))
         pairs = ctx.enter_context(tc.tile_pool(name="pairs", bufs=4))
+        scaled = ctx.enter_context(tc.tile_pool(name="scaled", bufs=1))
         late = ctx.enter_context(tc.tile_pool(name="late", bufs=ROW_TILES))
         relus = ctx.enter_context(tc.tile_pool(name="relus", bufs=3 * OUT_TILES))
         banks = ctx.enter_context(tc.psum_pool(name="banks", bufs=4))
-        groups = ctx.enter_context(tc.psum_pool(name="groups", bufs=2))
+        groups = ctx.enter_context(tc.psum_pool(name="groups", bufs=1))
+        givers = ctx.enter_context(tc.psum_pool(name="givers", bufs=2))
         ctx.enter_context(tc.manual_schedule())
 
         zeros = keep.tile([P, C], BF16)
@@ -61,12 +63,14 @@ def tile_nonlocalmp_pa_t_kernel(tc, F, W1_words, W1_scales, b1, W2_words, W2_sca
         f_tiled = f_rows.rearrange("(a p) c -> p a c", p=P)
         nc.sync.dma_start(out=f_sb[:, 0:1, :], in_=f_tiled[:, 0:1, :])
         b1_pt = keep.tile([P, PACK], BF16)
+        b1_cols = keep.tile([P, PACK], F32)
         nc.sync.dma_start(out=b1_pt[:], in_=b1.rearrange("(p t) -> p t", t=PACK))
         b2_rows = keep.tile([P, P], BF16)
         nc.vector.memset(b2_rows[:], 0.0)
         nc.sync.dma_start(out=b2_rows[0:OUT_TILES, :], in_=b2.rearrange("(n p) -> n p", p=P))
         w1 = keep.tile([P, 2, C], U32, align_bytes=64)
-        nc.sync.dma_start(out=w1[:].bitcast(I32), in_=W1_words.rearrange("g p n t -> p g (n t)").bitcast(I32))
+        for g in (1, 0):
+            nc.sync.dma_start(out=w1[:, g, :].bitcast(I32), in_=W1_words[g].rearrange("p n t -> p (n t)").bitcast(I32))
         for quad in range(4):
             nc.sync.dma_start(
                 out=w_planes[32 * quad : 32 * quad + 4, 0:2, :].bitcast(I32),
@@ -93,18 +97,20 @@ def tile_nonlocalmp_pa_t_kernel(tc, F, W1_words, W1_scales, b1, W2_words, W2_sca
         f_grp_words = f_grp[:].rearrange("p r t -> p (r t)").bitcast(F32).rearrange("p (r u) -> p r u", u=2)
         f_codes = keep.tile([P, ROWS], U32, align_bytes=64)
         f_scales = keep.tile([P, ROWS], U8, align_bytes=64)
-        a_t = keep.tile([P, ROW_TILES, P, PACK], F32)
-        b_t = keep.tile([P, ROW_TILES, NODES, TILE_SETS, PACK], F32)
-        sorted_ch = {}
-        b1_squares = keep.tile([P, PACK, P], F32)
-        b1_rows = keep.tile([P, PACK, P], F32)
+        b_t = keep.tile([P, ROW_TILES, PACK, NODES, TILE_SETS], F32)
+        a_ps = {}
+        w1_sorted = keep.tile([P, 2, PACK, P], U32, align_bytes=64)
+        w1_sorted_scales = keep.tile([P, 2, PACK, P], U8, align_bytes=64)
 
-        def spread_b1():
-            nc.vector.tensor_copy(out=b1_squares[:], in_=b1_pt[:].unsqueeze(2).to_broadcast([P, PACK, P]))
-            b1_ps = banks.tile([P, C], F32, name="b1_ps", tag="bank")
-            for t in range(PACK):
-                nc.tensor.transpose(b1_ps[:, t * P : (t + 1) * P], b1_squares[:, t, :], ident[:])
-            nc.vector.tensor_copy(out=b1_rows[:].rearrange("r t m -> r (t m)"), in_=b1_ps[:])
+        def sort_words(g):
+            nc.vector.tensor_copy(
+                out=w1_sorted[:, g].bitcast(I32), in_=w1[:, g, :].bitcast(I32).rearrange("p (m t) -> p t m", t=PACK)
+            )
+
+        def sort_scales(g):
+            nc.vector.tensor_copy(
+                out=w1_sorted_scales[:, g], in_=w_planes[:, g, :].rearrange("p (m t) -> p t m", t=PACK)
+            )
 
         def prepare_codes(a):
             rows = slice(a * P, (a + 1) * P)
@@ -122,65 +128,30 @@ def tile_nonlocalmp_pa_t_kernel(tc, F, W1_words, W1_scales, b1, W2_words, W2_sca
                 in_=f_grp[:, rows, :].rearrange("p r t -> p (r t)"),
             )
 
-        def prepare_products(a, shared=False):
+        def multiply_rows(a, g, bank):
             rows = slice(a * P, (a + 1) * P)
-            for g in range(2):
-                prod = banks.tile([P, C], F32, name="prod", tag="bank")
+            for t in range(PACK):
                 nc.tensor.matmul_mx(
-                    out=prod[:],
-                    lhsT=f_codes[:, rows].bitcast(FP8X4),
-                    lhsT_scale=f_scales[:, rows],
-                    rhs=w1[:, g, :].bitcast(FP8X4),
-                    rhs_scale=w_planes[:, g, :],
+                    out=bank[:, t * P : (t + 1) * P],
+                    lhsT=w1_sorted[:, g, t].bitcast(FP8X4),
+                    lhsT_scale=w1_sorted_scales[:, g, t],
+                    rhs=f_codes[:, rows].bitcast(FP8X4),
+                    rhs_scale=f_scales[:, rows],
                     start=True,
                     stop=True,
                 )
-                sorted_ch[a, g] = stage.tile([P, PACK, P], F32, name="sorted_ch", tag="sorted_ch")
-                if shared and g == 1:
-                    nc.vector.tensor_copy(out=sorted_ch[a, g][:], in_=prod[:].rearrange("r (m t) -> r t m", t=PACK))
-                else:
-                    nc.scalar.copy(out=sorted_ch[a, g][:], in_=prod[:].rearrange("r (m t) -> r t m", t=PACK))
 
-        def prepare_turned(a, shared=False):
-            turned_b = banks.tile([P, C], F32, name="turned_b", tag="bank")
+        def prepare_products(a, shared=False):
+            b_ps = banks.tile([P, C], F32, name="b_ps", tag="bank")
+            multiply_rows(a, 1, b_ps)
+            a_ps[a] = givers.tile([P, C], F32, name="a_ps", tag="a_ps")
+            multiply_rows(a, 0, a_ps[a])
             for t in range(PACK):
-                nc.tensor.matmul(
-                    out=turned_b[:, t * P : (t + 1) * P],
-                    lhsT=b1_rows[:, t, :],
-                    rhs=ident[:],
-                    is_transpose=True,
-                    start=(t == 0),
-                    stop=False,
-                )
-            turned_a = banks.tile([P, C], F32, name="turned_a", tag="bank")
-            for t in range(PACK):
-                nc.tensor.matmul(
-                    out=turned_a[:, t * P : (t + 1) * P],
-                    lhsT=sorted_ch[a, 0][:, t, :],
-                    rhs=ident[:],
-                    is_transpose=True,
-                    start=(t == 0),
-                    stop=(t == PACK - 1),
-                )
-            if shared:
-                nc.vector.tensor_copy(out=a_t[:, a], in_=turned_a[:].rearrange("p (t r) -> p r t", t=PACK))
-            else:
-                nc.scalar.copy(out=a_t[:, a], in_=turned_a[:].rearrange("p (t r) -> p r t", t=PACK))
-            for t in range(PACK):
-                nc.tensor.matmul(
-                    out=turned_b[:, t * P : (t + 1) * P],
-                    lhsT=sorted_ch[a, 1][:, t, :],
-                    rhs=ident[:],
-                    is_transpose=True,
-                    start=False,
-                    stop=(t == PACK - 1),
-                )
-            by_j = turned_b[:].rearrange("p (t b j) -> p j b t", t=PACK, j=NODES)
-            if shared:
-                nc.scalar.copy(out=b_t[:, a, 0:J_STEP], in_=by_j[:, 0:J_STEP])
-                nc.scalar.copy(out=b_t[:, a, J_STEP:NODES], in_=by_j[:, J_STEP:NODES])
-            else:
-                nc.scalar.copy(out=b_t[:, a], in_=by_j)
+                by_j = b_ps[:, t * P : (t + 1) * P].rearrange("p (b j) -> p j b", j=NODES)
+                if shared and t >= 2:
+                    nc.vector.tensor_scalar_add(out=b_t[:, a, t], in0=by_j, scalar1=b1_cols[:, t : t + 1])
+                else:
+                    nc.scalar.activation(out=b_t[:, a, t], in_=by_j, func=ACT.Identity, bias=b1_cols[:, t : t + 1])
 
         b2_square = keep.tile([P, P], F32)
         b2_pos = keep.tile([P, OUT_TILES], F32)
@@ -218,8 +189,8 @@ def tile_nonlocalmp_pa_t_kernel(tc, F, W1_words, W1_scales, b1, W2_words, W2_sca
             v[s] = pairs.tile([P, COLS * PACK], F32, name="v", tag="v")
             nc.vector.tensor_tensor(
                 out=v[s][:, 0 : width_of(s)].rearrange("p (j b i t) -> p j b i t", j=nj, b=TILE_SETS, i=NODES),
-                in0=a_t[:, a].rearrange("p (b i) t -> p b i t", i=NODES).unsqueeze(1).to_broadcast(shape),
-                in1=b_t[:, a, j0 : j0 + nj].unsqueeze(3).to_broadcast(shape),
+                in0=a_ps[a][:].rearrange("p (t b i) -> p b i t", t=PACK, i=NODES).unsqueeze(1).to_broadcast(shape),
+                in1=b_t[:, a, :, j0 : j0 + nj].rearrange("p t j b -> p j b t").unsqueeze(3).to_broadcast(shape),
                 op=ALU.add,
             )
 
@@ -237,9 +208,14 @@ def tile_nonlocalmp_pa_t_kernel(tc, F, W1_words, W1_scales, b1, W2_words, W2_sca
         def round_pairs(s):
             split = split_of(s)
             v_bf[s] = pairs.tile([P, split], BF16, name="v_bf", tag="v_bf")
-            w_bf[s] = pairs.tile([P, split], BF16, name="w_bf", tag="w_bf")
             nc.scalar.copy(out=v_bf[s][:], in_=v[s][:, 0:split])
-            nc.scalar.mul(out=w_bf[s][:], in_=v[s][:, 0:split], mul=NEG_SLOPE)
+
+        def scale_pairs(s):
+            split = split_of(s)
+            w_bf[s] = scaled.tile([P, split], BF16, name="w_bf", tag="w_bf")
+            nc.gpsimd.tensor_scalar(
+                out=w_bf[s][:], in0=v[s][:, 0:split], scalar1=NEG_SLOPE, scalar2=0.0, op0=ALU.mult, op1=ALU.add
+            )
 
         def leaky_of_roundings(s):
             split = split_of(s)
@@ -337,33 +313,41 @@ def tile_nonlocalmp_pa_t_kernel(tc, F, W1_words, W1_scales, b1, W2_words, W2_sca
             nc.vector.tensor_tensor(out=result[:], in0=pos[a][:], in1=base[a][:], op=ALU.add)
             nc.sync.dma_start(out=out_rows[a * P : (a + 1) * P, :], in_=result[:])
 
+        nc.vector.tensor_copy(out=b1_cols[:], in_=b1_pt[:])
         prepare_codes(0)
         quantise_rows(0)
-        spread_b1()
+        sort_words(1)
+        sort_words(0)
+        sort_scales(1)
+        sort_scales(0)
         spread_b2()
         prepare_products(0, shared=True)
-        prepare_turned(0, shared=True)
         prepare_codes(1)
         add_pairs(0)
         quantise_rows(1)
         prepare_products(1)
-        leaky_by_vector(0)
+        scale_pairs(0)
         round_pairs(0)
-        prepare_turned(1)
         add_pairs(1)
-        leaky_by_vector(1)
+        leaky_by_vector(0)
         round_pairs(1)
         leaky_of_roundings(0)
+        scale_pairs(1)
         add_pairs(2)
         quantise(0)
+        leaky_by_vector(1)
         leaky_by_vector(2)
         round_pairs(2)
 
         for s in range(len(steps) + 1):
             a, j0, nj = steps[s] if s < len(steps) else (ROW_TILES, 0, 0)
+            if 1 < s < len(steps) and steps[s - 2][0] < steps[s - 1][0]:
+                take_pos(steps[s - 2][0])
             q = j0 // J_STEP if nj == J_STEP else -1
             if s + 1 < len(steps):
                 leaky_of_roundings(s + 1)
+            if s + 2 < len(steps):
+                scale_pairs(s + 2)
             if s + LEAD < len(steps):
                 add_pairs(s + LEAD)
             if s + 1 < len(steps):
@@ -377,16 +361,12 @@ def tile_nonlocalmp_pa_t_kernel(tc, F, W1_words, W1_scales, b1, W2_words, W2_sca
                 quantise_rows(a + AHEAD)
             if a + AHEAD < ROW_TILES and q == 1:
                 prepare_products(a + AHEAD)
-            if a + AHEAD < ROW_TILES and q == 2:
-                prepare_turned(a + AHEAD)
             if s > 0:
                 add_up(s - 1)
             if s < len(steps) and j0 + nj == NODES:
                 scale_lin(a)
             if s + LEAD < len(steps):
                 round_pairs(s + LEAD)
-            if s > 0 and s - 1 < len(steps) and steps[s - 1][1] == 0 and steps[s - 1][0] > 0:
-                take_pos(steps[s - 1][0] - 1)
         for a in range(ROW_TILES - 1):
             finish_late(a)
         finish(ROW_TILES - 1)

@@ -25,7 +25,7 @@ OUT_TILES = C // P
 NEG_SLOPE = 0.2
 POS_SLOPE = 1.0 - NEG_SLOPE
 SHARE = 21
-WIDTHS = {ROW_TILES - 1: [2] * 8}
+WIDTHS = {0: [2, 2, 4, 4, 4], ROW_TILES - 1: [2] * 8}
 WARM_UP = 3
 LEAD = 3
 AHEAD = 2
@@ -62,20 +62,19 @@ def tile_nonlocalmp_pa_t_kernel(tc, F, W1_words, W1_scales, b1, W2_words, W2_sca
         f_sb = keep.tile([P, ROW_TILES, C], BF16)
         f_tiled = f_rows.rearrange("(a p) c -> p a c", p=P)
         nc.sync.dma_start(out=f_sb[:, 0:1, :], in_=f_tiled[:, 0:1, :])
-        b1_pt = keep.tile([P, PACK], BF16)
-        b1_cols = keep.tile([P, PACK], F32)
-        nc.sync.dma_start(out=b1_pt[:], in_=b1.rearrange("(p t) -> p t", t=PACK))
-        b2_rows = keep.tile([P, P], BF16)
-        nc.vector.memset(b2_rows[:], 0.0)
-        nc.sync.dma_start(out=b2_rows[0:OUT_TILES, :], in_=b2.rearrange("(n p) -> n p", p=P))
-        w1 = keep.tile([P, 2, C], U32, align_bytes=64)
-        for g in (1, 0):
-            nc.sync.dma_start(out=w1[:, g, :].bitcast(I32), in_=W1_words[g].rearrange("p n t -> p (n t)").bitcast(I32))
         for quad in range(4):
             nc.sync.dma_start(
                 out=w_planes[32 * quad : 32 * quad + 4, 0:2, :].bitcast(I32),
                 in_=W1_scales[:, 4 * quad : 4 * quad + 4, :].rearrange("g r n -> r g n").bitcast(I32),
             )
+        w1 = keep.tile([P, 2, C], U32, align_bytes=64)
+        for g in (1, 0):
+            nc.sync.dma_start(out=w1[:, g, :].bitcast(I32), in_=W1_words[g].rearrange("p n t -> p (n t)").bitcast(I32))
+        b1_pt = keep.tile([P, PACK], BF16)
+        nc.sync.dma_start(out=b1_pt[:], in_=b1.rearrange("(p t) -> p t", t=PACK))
+        b2_rows = keep.tile([P, P], BF16)
+        nc.vector.memset(b2_rows[:], 0.0)
+        nc.sync.dma_start(out=b2_rows[0:OUT_TILES, :], in_=b2.rearrange("(n p) -> n p", p=P))
         for quad in range(4):
             nc.sync.dma_start(
                 out=w_planes[32 * quad : 32 * quad + 4, 2, :].bitcast(I32),
@@ -128,11 +127,11 @@ def tile_nonlocalmp_pa_t_kernel(tc, F, W1_words, W1_scales, b1, W2_words, W2_sca
                 in_=f_grp[:, rows, :].rearrange("p r t -> p (r t)"),
             )
 
-        def multiply_rows(a, g, bank):
+        def multiply_rows(a, g, quarters):
             rows = slice(a * P, (a + 1) * P)
             for t in range(PACK):
                 nc.tensor.matmul_mx(
-                    out=bank[:, t * P : (t + 1) * P],
+                    out=quarters[t],
                     lhsT=w1_sorted[:, g, t].bitcast(FP8X4),
                     lhsT_scale=w1_sorted_scales[:, g, t],
                     rhs=f_codes[:, rows].bitcast(FP8X4),
@@ -141,17 +140,24 @@ def tile_nonlocalmp_pa_t_kernel(tc, F, W1_words, W1_scales, b1, W2_words, W2_sca
                     stop=True,
                 )
 
+        def quarters_of(bank):
+            return [bank[:, t * P : (t + 1) * P] for t in range(PACK)]
+
         def prepare_products(a, shared=False):
             b_ps = banks.tile([P, C], F32, name="b_ps", tag="bank")
-            multiply_rows(a, 1, b_ps)
+            quarters = quarters_of(b_ps)
+            if shared:
+                b_ps2 = banks.tile([P, C], F32, name="b_ps2", tag="bank")
+                quarters = quarters[0:2] + quarters_of(b_ps2)[0:2]
+            multiply_rows(a, 1, quarters)
             a_ps[a] = givers.tile([P, C], F32, name="a_ps", tag="a_ps")
-            multiply_rows(a, 0, a_ps[a])
+            multiply_rows(a, 0, quarters_of(a_ps[a]))
             for t in range(PACK):
-                by_j = b_ps[:, t * P : (t + 1) * P].rearrange("p (b j) -> p j b", j=NODES)
+                by_j = quarters[t].rearrange("p (b j) -> p j b", j=NODES)
                 if shared and t >= 2:
-                    nc.vector.tensor_scalar_add(out=b_t[:, a, t], in0=by_j, scalar1=b1_cols[:, t : t + 1])
+                    nc.vector.tensor_scalar_add(out=b_t[:, a, t], in0=by_j, scalar1=b1_pt[:, t : t + 1])
                 else:
-                    nc.scalar.activation(out=b_t[:, a, t], in_=by_j, func=ACT.Identity, bias=b1_cols[:, t : t + 1])
+                    nc.scalar.activation(out=b_t[:, a, t], in_=by_j, func=ACT.Identity, bias=b1_pt[:, t : t + 1])
 
         b2_square = keep.tile([P, P], F32)
         b2_pos = keep.tile([P, OUT_TILES], F32)
@@ -175,7 +181,7 @@ def tile_nonlocalmp_pa_t_kernel(tc, F, W1_words, W1_scales, b1, W2_words, W2_sca
                 j0 += width
 
         def split_of(s):
-            return SHARE * steps[s][2] * P // 32 * PACK
+            return 0 if s == 0 else (12 if steps[s][0] == ROW_TILES - 1 else SHARE) * steps[s][2] * P // 32 * PACK
 
         def width_of(s):
             return steps[s][2] * P * PACK
@@ -213,9 +219,12 @@ def tile_nonlocalmp_pa_t_kernel(tc, F, W1_words, W1_scales, b1, W2_words, W2_sca
         def scale_pairs(s):
             split = split_of(s)
             w_bf[s] = scaled.tile([P, split], BF16, name="w_bf", tag="w_bf")
-            nc.gpsimd.tensor_scalar(
-                out=w_bf[s][:], in0=v[s][:, 0:split], scalar1=NEG_SLOPE, scalar2=0.0, op0=ALU.mult, op1=ALU.add
-            )
+            if s == 1:
+                nc.scalar.mul(out=w_bf[s][:], in_=v[s][:, 0:split], mul=NEG_SLOPE)
+            else:
+                nc.gpsimd.tensor_scalar(
+                    out=w_bf[s][:], in0=v[s][:, 0:split], scalar1=NEG_SLOPE, scalar2=0.0, op0=ALU.mult, op1=ALU.add
+                )
 
         def leaky_of_roundings(s):
             split = split_of(s)
@@ -313,37 +322,30 @@ def tile_nonlocalmp_pa_t_kernel(tc, F, W1_words, W1_scales, b1, W2_words, W2_sca
             nc.vector.tensor_tensor(out=result[:], in0=pos[a][:], in1=base[a][:], op=ALU.add)
             nc.sync.dma_start(out=out_rows[a * P : (a + 1) * P, :], in_=result[:])
 
-        nc.vector.tensor_copy(out=b1_cols[:], in_=b1_pt[:])
         prepare_codes(0)
-        quantise_rows(0)
-        sort_words(1)
-        sort_words(0)
         sort_scales(1)
+        sort_words(1)
+        quantise_rows(0)
         sort_scales(0)
-        spread_b2()
+        sort_words(0)
         prepare_products(0, shared=True)
+        spread_b2()
         prepare_codes(1)
         add_pairs(0)
-        quantise_rows(1)
-        prepare_products(1)
-        scale_pairs(0)
-        round_pairs(0)
-        add_pairs(1)
         leaky_by_vector(0)
-        round_pairs(1)
-        leaky_of_roundings(0)
-        scale_pairs(1)
-        add_pairs(2)
+        add_pairs(1)
         quantise(0)
+        scale_pairs(1)
+        round_pairs(1)
         leaky_by_vector(1)
+        quantise_rows(1)
+        add_pairs(2)
         leaky_by_vector(2)
-        round_pairs(2)
 
         for s in range(len(steps) + 1):
             a, j0, nj = steps[s] if s < len(steps) else (ROW_TILES, 0, 0)
             if 1 < s < len(steps) and steps[s - 2][0] < steps[s - 1][0]:
                 take_pos(steps[s - 2][0])
-            q = j0 // J_STEP if nj == J_STEP else -1
             if s + 1 < len(steps):
                 leaky_of_roundings(s + 1)
             if s + 2 < len(steps):
@@ -356,10 +358,13 @@ def tile_nonlocalmp_pa_t_kernel(tc, F, W1_words, W1_scales, b1, W2_words, W2_sca
                 leaky_by_vector(s + LEAD)
             if s < len(steps):
                 relu(s, multiply(s))
-            if a + AHEAD < ROW_TILES and q == 0:
+            if s == 0:
+                prepare_products(1)
+                round_pairs(2)
+            if a + AHEAD < ROW_TILES and j0 == J_STEP:
                 prepare_codes(a + AHEAD)
                 quantise_rows(a + AHEAD)
-            if a + AHEAD < ROW_TILES and q == 1:
+            if a + AHEAD < ROW_TILES and j0 == 2 * J_STEP:
                 prepare_products(a + AHEAD)
             if s > 0:
                 add_up(s - 1)

@@ -24,7 +24,7 @@ COLS = J_STEP * P
 OUT_TILES = C // P
 NEG_SLOPE = 0.2
 POS_SLOPE = 1.0 - NEG_SLOPE
-SHARE = 21
+SHARE = 23
 WIDTHS = {0: [2, 2, 4, 4, 4], ROW_TILES - 1: [2] * 8}
 WARM_UP = 3
 LEAD = 3
@@ -181,7 +181,7 @@ def tile_nonlocalmp_pa_t_kernel(tc, F, W1_words, W1_scales, b1, W2_words, W2_sca
                 j0 += width
 
         def split_of(s):
-            return 0 if s == 0 else (12 if steps[s][0] == ROW_TILES - 1 else SHARE) * steps[s][2] * P // 32 * PACK
+            return 0 if s == 0 else SHARE * steps[s][2] * P // 32 * PACK
 
         def width_of(s):
             return steps[s][2] * P * PACK

@@ -24,8 +24,9 @@ COLS = J_STEP * P
 OUT_TILES = C // P
 NEG_SLOPE = 0.2
 POS_SLOPE = 1.0 - NEG_SLOPE
-SHARE = 23
-WIDTHS = {0: [2, 2, 4, 4, 4], ROW_TILES - 1: [2] * 8}
+SHARE = 24
+WIDTHS = {0: [2, 2, 4, 4, 4], ROW_TILES - 1: [4, 4, 4, 2, 2]}
+ALONE = 5
 WARM_UP = 3
 LEAD = 3
 AHEAD = 2
@@ -40,7 +41,7 @@ def tile_nonlocalmp_pa_t_kernel(tc, F, W1_words, W1_scales, b1, W2_words, W2_sca
 
     with ExitStack() as ctx:
         keep = ctx.enter_context(tc.tile_pool(name="keep", bufs=1))
-        stage = ctx.enter_context(tc.tile_pool(name="stage", bufs=4))
+        stage = ctx.enter_context(tc.tile_pool(name="stage", bufs=ROW_TILES))
         pairs = ctx.enter_context(tc.tile_pool(name="pairs", bufs=4))
         scaled = ctx.enter_context(tc.tile_pool(name="scaled", bufs=1))
         late = ctx.enter_context(tc.tile_pool(name="late", bufs=ROW_TILES))
@@ -111,13 +112,17 @@ def tile_nonlocalmp_pa_t_kernel(tc, F, W1_words, W1_scales, b1, W2_words, W2_sca
                 out=w1_sorted_scales[:, g], in_=w_planes[:, g, :].rearrange("p (m t) -> p t m", t=PACK)
             )
 
-        def prepare_codes(a):
-            rows = slice(a * P, (a + 1) * P)
-            f_words = f_sb[:, a, :].bitcast(F32)
-            f_ps = banks.tile([P, C], F32, name="f_ps", tag="bank")
-            for u in range(2):
-                nc.tensor.transpose(f_ps[:, u * P : (u + 1) * P], f_words[:, u : C // 2 : 2], ident[:])
-            nc.scalar.copy(out=f_grp_words[:, rows, :], in_=f_ps[:, 0 : 2 * P].rearrange("p (u r) -> p r u", u=2))
+        def prepare_codes(first, count=1):
+            rows = slice(first * P, (first + count) * P)
+            f_ps = banks.tile([P, 2, 2, P], F32, name="f_ps", tag="bank")
+            for a in range(count):
+                f_words = f_sb[:, first + a, :].bitcast(F32)
+                for u in range(2):
+                    nc.tensor.transpose(f_ps[:, a, u, :], f_words[:, u : C // 2 : 2], ident[:])
+            nc.scalar.copy(
+                out=f_grp_words[:, rows, :].rearrange("p (a r) u -> p a r u", a=count),
+                in_=f_ps[:, 0:count].rearrange("p a u r -> p a r u"),
+            )
 
         def quantise_rows(a):
             rows = slice(a * P, (a + 1) * P)
@@ -180,8 +185,14 @@ def tile_nonlocalmp_pa_t_kernel(tc, F, W1_words, W1_scales, b1, W2_words, W2_sca
                 steps.append((a, j0, width))
                 j0 += width
 
+        def alone(s):
+            return s == 0 or s >= len(steps) - ALONE
+
+        def lead_of(s):
+            return LEAD - 1 if s > len(steps) - ALONE else LEAD
+
         def split_of(s):
-            return 0 if s == 0 else SHARE * steps[s][2] * P // 32 * PACK
+            return 0 if alone(s) else SHARE * steps[s][2] * P // 32 * PACK
 
         def width_of(s):
             return steps[s][2] * P * PACK
@@ -219,12 +230,9 @@ def tile_nonlocalmp_pa_t_kernel(tc, F, W1_words, W1_scales, b1, W2_words, W2_sca
         def scale_pairs(s):
             split = split_of(s)
             w_bf[s] = scaled.tile([P, split], BF16, name="w_bf", tag="w_bf")
-            if s == 1:
-                nc.scalar.mul(out=w_bf[s][:], in_=v[s][:, 0:split], mul=NEG_SLOPE)
-            else:
-                nc.gpsimd.tensor_scalar(
-                    out=w_bf[s][:], in0=v[s][:, 0:split], scalar1=NEG_SLOPE, scalar2=0.0, op0=ALU.mult, op1=ALU.add
-                )
+            nc.gpsimd.tensor_scalar(
+                out=w_bf[s][:], in0=v[s][:, 0:split], scalar1=NEG_SLOPE, scalar2=0.0, op0=ALU.mult, op1=ALU.add
+            )
 
         def leaky_of_roundings(s):
             split = split_of(s)
@@ -324,45 +332,47 @@ def tile_nonlocalmp_pa_t_kernel(tc, F, W1_words, W1_scales, b1, W2_words, W2_sca
 
         prepare_codes(0)
         sort_scales(1)
+        sort_scales(0)
         sort_words(1)
         quantise_rows(0)
-        sort_scales(0)
         sort_words(0)
         prepare_products(0, shared=True)
         spread_b2()
         prepare_codes(1)
+        for a in range(2, ROW_TILES, 2):
+            prepare_codes(a, 2)
         add_pairs(0)
         leaky_by_vector(0)
         add_pairs(1)
         quantise(0)
         scale_pairs(1)
         round_pairs(1)
+        add_pairs(2)
         leaky_by_vector(1)
         quantise_rows(1)
-        add_pairs(2)
         leaky_by_vector(2)
 
         for s in range(len(steps) + 1):
             a, j0, nj = steps[s] if s < len(steps) else (ROW_TILES, 0, 0)
             if 1 < s < len(steps) and steps[s - 2][0] < steps[s - 1][0]:
                 take_pos(steps[s - 2][0])
-            if s + 1 < len(steps):
+            ahead = [t for t in range(s + LEAD - 1, min(s + LEAD + 1, len(steps))) if t - lead_of(t) == s]
+            if s + 1 < len(steps) and not alone(s + 1):
                 leaky_of_roundings(s + 1)
-            if s + 2 < len(steps):
+            if s + 2 < len(steps) and not alone(s + 2):
                 scale_pairs(s + 2)
-            if s + LEAD < len(steps):
-                add_pairs(s + LEAD)
+            for t in ahead:
+                add_pairs(t)
             if s + 1 < len(steps):
                 quantise(s + 1)
-            if s + LEAD < len(steps):
-                leaky_by_vector(s + LEAD)
+            for t in ahead:
+                leaky_by_vector(t)
             if s < len(steps):
                 relu(s, multiply(s))
             if s == 0:
-                prepare_products(1)
                 round_pairs(2)
+                prepare_products(1)
             if a + AHEAD < ROW_TILES and j0 == J_STEP:
-                prepare_codes(a + AHEAD)
                 quantise_rows(a + AHEAD)
             if a + AHEAD < ROW_TILES and j0 == 2 * J_STEP:
                 prepare_products(a + AHEAD)
@@ -370,7 +380,7 @@ def tile_nonlocalmp_pa_t_kernel(tc, F, W1_words, W1_scales, b1, W2_words, W2_sca
                 add_up(s - 1)
             if s < len(steps) and j0 + nj == NODES:
                 scale_lin(a)
-            if s + LEAD < len(steps):
+            if s + LEAD < len(steps) and not alone(s + LEAD):
                 round_pairs(s + LEAD)
         for a in range(ROW_TILES - 1):
             finish_late(a)

@@ -25,10 +25,9 @@ OUT_TILES = C // P
 NEG_SLOPE = 0.2
 POS_SLOPE = 1.0 - NEG_SLOPE
 SHARE = 24
-WIDTHS = {0: [2, 2, 4, 4, 4], ROW_TILES - 1: [4, 4, 4, 2, 2]}
-ALONE = 5
+WIDTHS = {0: [2, 2, 4, 4, 4]}
 WARM_UP = 3
-LEAD = 3
+LEAD = 2
 AHEAD = 2
 
 FLOPS = 2 * ROWS * (2 * C) * C + 2 * SETS * NODES * NODES * C * C
@@ -43,7 +42,6 @@ def tile_nonlocalmp_pa_t_kernel(tc, F, W1_words, W1_scales, b1, W2_words, W2_sca
         keep = ctx.enter_context(tc.tile_pool(name="keep", bufs=1))
         stage = ctx.enter_context(tc.tile_pool(name="stage", bufs=ROW_TILES))
         pairs = ctx.enter_context(tc.tile_pool(name="pairs", bufs=4))
-        scaled = ctx.enter_context(tc.tile_pool(name="scaled", bufs=1))
         late = ctx.enter_context(tc.tile_pool(name="late", bufs=ROW_TILES))
         relus = ctx.enter_context(tc.tile_pool(name="relus", bufs=3 * OUT_TILES))
         banks = ctx.enter_context(tc.psum_pool(name="banks", bufs=4))
@@ -124,8 +122,8 @@ def tile_nonlocalmp_pa_t_kernel(tc, F, W1_words, W1_scales, b1, W2_words, W2_sca
                 in_=f_ps[:, 0:count].rearrange("p a u r -> p a r u"),
             )
 
-        def quantise_rows(a):
-            rows = slice(a * P, (a + 1) * P)
+        def quantise_rows(first, count=1):
+            rows = slice(first * P, (first + count) * P)
             nc.vector.quantize_mx(
                 out=f_codes[:, rows].bitcast(FP8X4),
                 scales=f_scales[:, rows],
@@ -185,18 +183,13 @@ def tile_nonlocalmp_pa_t_kernel(tc, F, W1_words, W1_scales, b1, W2_words, W2_sca
                 steps.append((a, j0, width))
                 j0 += width
 
-        def alone(s):
-            return s == 0 or s >= len(steps) - ALONE
-
-        def lead_of(s):
-            return LEAD - 1 if s > len(steps) - ALONE else LEAD
-
         def split_of(s):
-            return 0 if alone(s) else SHARE * steps[s][2] * P // 32 * PACK
+            return 0 if s == 0 else SHARE * steps[s][2] * P // 32 * PACK
 
         def width_of(s):
             return steps[s][2] * P * PACK
         v, h, v_bf, w_bf, codes, scales, r = {}, {}, {}, {}, {}, {}, {}
+        pos_bank = {}
         lin, pos = {}, {}
         base = {}
 
@@ -229,14 +222,14 @@ def tile_nonlocalmp_pa_t_kernel(tc, F, W1_words, W1_scales, b1, W2_words, W2_sca
 
         def scale_pairs(s):
             split = split_of(s)
-            w_bf[s] = scaled.tile([P, split], BF16, name="w_bf", tag="w_bf")
+            w_bf[s] = h[s - 1][:, 0:split]
             nc.gpsimd.tensor_scalar(
-                out=w_bf[s][:], in0=v[s][:, 0:split], scalar1=NEG_SLOPE, scalar2=0.0, op0=ALU.mult, op1=ALU.add
+                out=w_bf[s], in0=v[s][:, 0:split], scalar1=NEG_SLOPE, scalar2=0.0, op0=ALU.mult, op1=ALU.add
             )
 
         def leaky_of_roundings(s):
             split = split_of(s)
-            nc.vector.tensor_tensor(out=h[s][:, 0:split], in0=v_bf[s][:], in1=w_bf[s][:], op=ALU.max)
+            nc.vector.tensor_tensor(out=h[s][:, 0:split], in0=v_bf[s][:], in1=w_bf[s], op=ALU.max)
 
         def quantise(s):
             codes[s] = pairs.tile([P, COLS], U32, name="codes", tag="codes", align_bytes=64)
@@ -288,26 +281,30 @@ def tile_nonlocalmp_pa_t_kernel(tc, F, W1_words, W1_scales, b1, W2_words, W2_sca
 
         def add_up(s):
             a, j0, nj = steps[s]
+            split = a == ROW_TILES - 1
             if j0 == 0:
-                pos[a] = groups.tile([P, C], F32, name="pos", tag="pos")
+                first = groups.tile([P, C], F32, name="pos", tag="pos")
+                second = givers.tile([P, C], F32, name="pos_too", tag="a_ps") if split else first
+                pos[a] = [(first if n < 2 else second)[:, n * P : (n + 1) * P] for n in range(OUT_TILES)]
+                pos_bank[a] = [first, second]
                 for n in range(OUT_TILES):
                     nc.tensor.matmul(
-                        out=pos[a][:, n * P : (n + 1) * P],
+                        out=pos[a][n],
                         lhsT=b2_squares[:, n, :],
                         rhs=ident[:],
                         is_transpose=True,
-                        start=(n == 0),
+                        start=(n == 0 or (split and n == 2)),
                         stop=False,
                     )
             for n in range(OUT_TILES):
                 for j in range(nj):
                     nc.tensor.matmul(
-                        out=pos[a][:, n * P : (n + 1) * P],
+                        out=pos[a][n],
                         lhsT=r[s][n][:, j * P : (j + 1) * P],
                         rhs=ident[:],
                         is_transpose=True,
                         start=False,
-                        stop=(j0 + nj == NODES and n == OUT_TILES - 1 and j == nj - 1),
+                        stop=(j0 + nj == NODES and j == nj - 1 and (n == OUT_TILES - 1 or (split and n == 1))),
                     )
 
         def scale_lin(a):
@@ -318,7 +315,7 @@ def tile_nonlocalmp_pa_t_kernel(tc, F, W1_words, W1_scales, b1, W2_words, W2_sca
 
         def take_pos(a):
             pos_sb[a] = late.tile([P, C], F32, name="pos_sb", tag="pos_sb")
-            nc.scalar.copy(out=pos_sb[a][:], in_=pos[a][:])
+            nc.scalar.copy(out=pos_sb[a][:], in_=pos_bank[a][0][:])
 
         def finish_late(a):
             result = stage.tile([P, C], F32, name="result", tag="result")
@@ -327,8 +324,12 @@ def tile_nonlocalmp_pa_t_kernel(tc, F, W1_words, W1_scales, b1, W2_words, W2_sca
 
         def finish(a):
             result = stage.tile([P, C], F32, name="result", tag="result")
-            nc.vector.tensor_tensor(out=result[:], in0=pos[a][:], in1=base[a][:], op=ALU.add)
-            nc.sync.dma_start(out=out_rows[a * P : (a + 1) * P, :], in_=result[:])
+            for half in range(2):
+                chans = slice(half * C // 2, (half + 1) * C // 2)
+                nc.vector.tensor_tensor(
+                    out=result[:, chans], in0=pos_bank[a][half][:, chans], in1=base[a][:, chans], op=ALU.add
+                )
+                nc.sync.dma_start(out=out_rows[a * P : (a + 1) * P, chans], in_=result[:, chans])
 
         prepare_codes(0)
         sort_scales(1)
@@ -345,42 +346,39 @@ def tile_nonlocalmp_pa_t_kernel(tc, F, W1_words, W1_scales, b1, W2_words, W2_sca
         leaky_by_vector(0)
         add_pairs(1)
         quantise(0)
-        scale_pairs(1)
         round_pairs(1)
-        add_pairs(2)
-        leaky_by_vector(1)
-        quantise_rows(1)
-        leaky_by_vector(2)
 
         for s in range(len(steps) + 1):
             a, j0, nj = steps[s] if s < len(steps) else (ROW_TILES, 0, 0)
             if 1 < s < len(steps) and steps[s - 2][0] < steps[s - 1][0]:
                 take_pos(steps[s - 2][0])
-            ahead = [t for t in range(s + LEAD - 1, min(s + LEAD + 1, len(steps))) if t - lead_of(t) == s]
-            if s + 1 < len(steps) and not alone(s + 1):
+            if s + 1 < len(steps):
+                scale_pairs(s + 1)
+            if s + LEAD < len(steps):
+                add_pairs(s + LEAD)
+            if s == 0:
+                leaky_by_vector(1)
+                quantise_rows(1)
+            if s + 1 < len(steps):
                 leaky_of_roundings(s + 1)
-            if s + 2 < len(steps) and not alone(s + 2):
-                scale_pairs(s + 2)
-            for t in ahead:
-                add_pairs(t)
+            if s + LEAD < len(steps):
+                leaky_by_vector(s + LEAD)
             if s + 1 < len(steps):
                 quantise(s + 1)
-            for t in ahead:
-                leaky_by_vector(t)
             if s < len(steps):
                 relu(s, multiply(s))
             if s == 0:
-                round_pairs(2)
                 prepare_products(1)
             if a + AHEAD < ROW_TILES and j0 == J_STEP:
-                quantise_rows(a + AHEAD)
+                if a % 2 == 0:
+                    quantise_rows(a + AHEAD, 2)
             if a + AHEAD < ROW_TILES and j0 == 2 * J_STEP:
                 prepare_products(a + AHEAD)
             if s > 0:
                 add_up(s - 1)
             if s < len(steps) and j0 + nj == NODES:
                 scale_lin(a)
-            if s + LEAD < len(steps) and not alone(s + LEAD):
+            if s + LEAD < len(steps):
                 round_pairs(s + LEAD)
         for a in range(ROW_TILES - 1):
             finish_late(a)

@@ -24,9 +24,10 @@ COLS = J_STEP * P
 OUT_TILES = C // P
 NEG_SLOPE = 0.2
 POS_SLOPE = 1.0 - NEG_SLOPE
-SHARE = 24
-WIDTHS = {0: [2, 2, 4, 4, 4]}
+SHARE = 23
+WIDTHS = {0: [2, 2, 4, 4, 4], ROW_TILES - 1: [4, 4, 4, 2, 2]}
 WARM_UP = 3
+ALONE = 3
 LEAD = 2
 AHEAD = 2
 
@@ -184,7 +185,7 @@ def tile_nonlocalmp_pa_t_kernel(tc, F, W1_words, W1_scales, b1, W2_words, W2_sca
                 j0 += width
 
         def split_of(s):
-            return 0 if s == 0 else SHARE * steps[s][2] * P // 32 * PACK
+            return 0 if s == 0 or s >= len(steps) - ALONE else SHARE * steps[s][2] * P // 32 * PACK
 
         def width_of(s):
             return steps[s][2] * P * PACK
@@ -352,19 +353,22 @@ def tile_nonlocalmp_pa_t_kernel(tc, F, W1_words, W1_scales, b1, W2_words, W2_sca
             a, j0, nj = steps[s] if s < len(steps) else (ROW_TILES, 0, 0)
             if 1 < s < len(steps) and steps[s - 2][0] < steps[s - 1][0]:
                 take_pos(steps[s - 2][0])
-            if s + 1 < len(steps):
+            if s + 1 < len(steps) and split_of(s + 1):
                 scale_pairs(s + 1)
             if s + LEAD < len(steps):
                 add_pairs(s + LEAD)
             if s == 0:
                 leaky_by_vector(1)
                 quantise_rows(1)
-            if s + 1 < len(steps):
+            if s + 1 < len(steps) and split_of(s + 1):
                 leaky_of_roundings(s + 1)
-            if s + LEAD < len(steps):
+            deferred = s + LEAD < len(steps) and not split_of(s + LEAD)
+            if s + LEAD < len(steps) and not deferred:
                 leaky_by_vector(s + LEAD)
             if s + 1 < len(steps):
                 quantise(s + 1)
+            if deferred:
+                leaky_by_vector(s + LEAD)
             if s < len(steps):
                 relu(s, multiply(s))
             if s == 0:
@@ -378,7 +382,7 @@ def tile_nonlocalmp_pa_t_kernel(tc, F, W1_words, W1_scales, b1, W2_words, W2_sca
                 add_up(s - 1)
             if s < len(steps) and j0 + nj == NODES:
                 scale_lin(a)
-            if s + LEAD < len(steps):
+            if s + LEAD < len(steps) and split_of(s + LEAD):
                 round_pairs(s + LEAD)
         for a in range(ROW_TILES - 1):
             finish_late(a)

@@ -27,6 +27,7 @@ POS_SLOPE = 1.0 - NEG_SLOPE
 SHARE = 23
 WIDTHS = {0: [2, 2, 4, 4, 4], ROW_TILES - 1: [4, 4, 4, 2, 2]}
 WARM_UP = 3
+V_WIDTH = max(COLS * PACK, SHARE * COLS * PACK // 32 * 3 // 2)
 ALONE = 3
 LEAD = 2
 AHEAD = 2
@@ -197,7 +198,7 @@ def tile_nonlocalmp_pa_t_kernel(tc, F, W1_words, W1_scales, b1, W2_words, W2_sca
         def add_pairs(s):
             a, j0, nj = steps[s]
             shape = [P, nj, TILE_SETS, NODES, PACK]
-            v[s] = pairs.tile([P, COLS * PACK], F32, name="v", tag="v")
+            v[s] = pairs.tile([P, V_WIDTH], F32, name="v", tag="v")
             nc.vector.tensor_tensor(
                 out=v[s][:, 0 : width_of(s)].rearrange("p (j b i t) -> p j b i t", j=nj, b=TILE_SETS, i=NODES),
                 in0=a_ps[a][:].rearrange("p (t b i) -> p b i t", t=PACK, i=NODES).unsqueeze(1).to_broadcast(shape),
@@ -223,7 +224,10 @@ def tile_nonlocalmp_pa_t_kernel(tc, F, W1_words, W1_scales, b1, W2_words, W2_sca
 
         def scale_pairs(s):
             split = split_of(s)
-            w_bf[s] = h[s - 1][:, 0:split]
+            if s == 1:
+                w_bf[s] = h[0][:, 0:split]
+            else:
+                w_bf[s] = v[s][:].bitcast(BF16)[:, 2 * split : 3 * split]
             nc.gpsimd.tensor_scalar(
                 out=w_bf[s], in0=v[s][:, 0:split], scalar1=NEG_SLOPE, scalar2=0.0, op0=ALU.mult, op1=ALU.add
             )

@@ -63,14 +63,18 @@ def tile_nonlocalmp_pa_t_kernel(tc, F, W1_words, W1_scales, b1, W2_words, W2_sca
         f_sb = keep.tile([P, ROW_TILES, C], BF16)
         f_tiled = f_rows.rearrange("(a p) c -> p a c", p=P)
         nc.sync.dma_start(out=f_sb[:, 0:1, :], in_=f_tiled[:, 0:1, :])
+        w1 = keep.tile([P, 2, C], U32, align_bytes=64)
+
+        def load_words(g):
+            nc.sync.dma_start(out=w1[:, g, :].bitcast(I32), in_=W1_words[g].rearrange("p n t -> p (n t)").bitcast(I32))
+
+        load_words(1)
         for quad in range(4):
             nc.sync.dma_start(
                 out=w_planes[32 * quad : 32 * quad + 4, 0:2, :].bitcast(I32),
                 in_=W1_scales[:, 4 * quad : 4 * quad + 4, :].rearrange("g r n -> r g n").bitcast(I32),
             )
-        w1 = keep.tile([P, 2, C], U32, align_bytes=64)
-        for g in (1, 0):
-            nc.sync.dma_start(out=w1[:, g, :].bitcast(I32), in_=W1_words[g].rearrange("p n t -> p (n t)").bitcast(I32))
+        load_words(0)
         b1_pt = keep.tile([P, PACK], BF16)
         nc.sync.dma_start(out=b1_pt[:], in_=b1.rearrange("(p t) -> p t", t=PACK))
         b2_rows = keep.tile([P, P], BF16)
@@ -107,9 +111,9 @@ def tile_nonlocalmp_pa_t_kernel(tc, F, W1_words, W1_scales, b1, W2_words, W2_sca
                 out=w1_sorted[:, g].bitcast(I32), in_=w1[:, g, :].bitcast(I32).rearrange("p (m t) -> p t m", t=PACK)
             )
 
-        def sort_scales(g):
+        def sort_scales():
             nc.vector.tensor_copy(
-                out=w1_sorted_scales[:, g], in_=w_planes[:, g, :].rearrange("p (m t) -> p t m", t=PACK)
+                out=w1_sorted_scales[:], in_=w_planes[:, 0:2, :].rearrange("p g (m t) -> p g t m", t=PACK)
             )
 
         def prepare_codes(first, count=1):
@@ -334,12 +338,11 @@ def tile_nonlocalmp_pa_t_kernel(tc, F, W1_words, W1_scales, b1, W2_words, W2_sca
                 nc.vector.tensor_tensor(
                     out=result[:, chans], in0=pos_bank[a][half][:, chans], in1=base[a][:, chans], op=ALU.add
                 )
-                nc.sync.dma_start(out=out_rows[a * P : (a + 1) * P, chans], in_=result[:, chans])
+                nc.scalar.dma_start(out=out_rows[a * P : (a + 1) * P, chans], in_=result[:, chans])
 
         prepare_codes(0)
-        sort_scales(1)
-        sort_scales(0)
         sort_words(1)
+        sort_scales()
         quantise_rows(0)
         sort_words(0)
         prepare_products(0, shared=True)
@@ -382,7 +385,9 @@ def tile_nonlocalmp_pa_t_kernel(tc, F, W1_words, W1_scales, b1, W2_words, W2_sca
                     quantise_rows(a + AHEAD, 2)
             if a + AHEAD < ROW_TILES and j0 == 2 * J_STEP:
                 prepare_products(a + AHEAD)
-            if s > 0:
+            if s == len(steps) - 1:
+                add_up(s - 2)
+            if s > 0 and s != len(steps) - 2:
                 add_up(s - 1)
             if s < len(steps) and j0 + nj == NODES:
                 scale_lin(a)

from contextlib import ExitStack

import concourse.mybir as mybir
from concourse.masks import make_identity

F32 = mybir.dt.float32
BF16 = mybir.dt.bfloat16
I32 = mybir.dt.int32
U32 = mybir.dt.uint32
U8 = mybir.dt.uint8
FP8X4 = mybir.dt.float8_e4m3fn_x4
ALU = mybir.AluOpType
ACT = mybir.ActivationFunctionType

P = 128
PACK = 4
SETS, NODES, C = 64, 16, 512
ROWS = SETS * NODES
ROW_TILES = ROWS // P
TILE_SETS = P // NODES
J_STEP = 4
STEPS_PER_TILE = NODES // J_STEP
COLS = J_STEP * P
OUT_TILES = C // P
NEG_SLOPE = 0.2
POS_SLOPE = 1.0 - NEG_SLOPE
SHARE = 23
WIDTHS = {0: [2, 2, 4, 4, 4], ROW_TILES - 1: [4, 4, 4, 2, 2]}
WARM_UP = 3
V_WIDTH = max(COLS * PACK, SHARE * COLS * PACK // 32 * 3 // 2)
ALONE = 3
LEAD = 2
AHEAD = 2

FLOPS = 2 * ROWS * (2 * C) * C + 2 * SETS * NODES * NODES * C * C


def tile_nonlocalmp_pa_t_kernel(tc, F, W1_words, W1_scales, b1, W2_words, W2_scales, b2, out):
    nc = tc.nc
    f_rows = F.flatten_outer_dims()
    out_rows = out.flatten_outer_dims()

    with ExitStack() as ctx:
        keep = ctx.enter_context(tc.tile_pool(name="keep", bufs=1))
        stage = ctx.enter_context(tc.tile_pool(name="stage", bufs=ROW_TILES))
        pairs = ctx.enter_context(tc.tile_pool(name="pairs", bufs=4))
        late = ctx.enter_context(tc.tile_pool(name="late", bufs=ROW_TILES))
        relus = ctx.enter_context(tc.tile_pool(name="relus", bufs=3 * OUT_TILES))
        banks = ctx.enter_context(tc.psum_pool(name="banks", bufs=4))
        groups = ctx.enter_context(tc.psum_pool(name="groups", bufs=1))
        givers = ctx.enter_context(tc.psum_pool(name="givers", bufs=2))
        ctx.enter_context(tc.manual_schedule())

        zeros = keep.tile([P, C], BF16)
        nc.gpsimd.memset(zeros[:], 0.0)
        spare = banks.tile([P, C], F32, name="spare", tag="bank")
        for k in range(WARM_UP):
            nc.tensor.matmul(out=spare[:], lhsT=zeros[:, 0:P], rhs=zeros[:], start=True, stop=True)

        w_planes = keep.tile([P, 3, C], U8, align_bytes=64)
        nc.vector.memset(w_planes[:].rearrange("p g n -> p (g n)").bitcast(I32), 0)

        f_sb = keep.tile([P, ROW_TILES, C], BF16)
        f_tiled = f_rows.rearrange("(a p) c -> p a c", p=P)
        nc.sync.dma_start(out=f_sb[:, 0:1, :], in_=f_tiled[:, 0:1, :])
        w1 = keep.tile([P, 2, C], U32, align_bytes=64)

        def load_words(g):
            nc.sync.dma_start(out=w1[:, g, :].bitcast(I32), in_=W1_words[g].rearrange("p n t -> p (n t)").bitcast(I32))

        load_words(1)
        for quad in range(4):
            nc.sync.dma_start(
                out=w_planes[32 * quad : 32 * quad + 4, 0:2, :].bitcast(I32),
                in_=W1_scales[:, 4 * quad : 4 * quad + 4, :].rearrange("g r n -> r g n").bitcast(I32),
            )
        load_words(0)
        b1_pt = keep.tile([P, PACK], BF16)
        nc.sync.dma_start(out=b1_pt[:], in_=b1.rearrange("(p t) -> p t", t=PACK))
        b2_rows = keep.tile([P, P], BF16)
        nc.vector.memset(b2_rows[:], 0.0)
        nc.sync.dma_start(out=b2_rows[0:OUT_TILES, :], in_=b2.rearrange("(n p) -> n p", p=P))
        for quad in range(4):
            nc.sync.dma_start(
                out=w_planes[32 * quad : 32 * quad + 4, 2, :].bitcast(I32),
                in_=W2_scales[0, 4 * quad : 4 * quad + 4, :].bitcast(I32),
            )
        w2 = keep.tile([P, C], U32, align_bytes=64)
        nc.sync.dma_start(out=w2[:].bitcast(I32), in_=W2_words[0].rearrange("p n t -> p (n t)").bitcast(I32))
        nc.sync.dma_start(out=f_sb[:, 1:2, :], in_=f_tiled[:, 1:2, :])
        nc.sync.dma_start(out=f_sb[:, 2:ROW_TILES, :], in_=f_tiled[:, 2:ROW_TILES, :])

        ident = keep.tile([P, P], F32)
        make_identity(nc, ident[:])

        warm = keep.tile([P, 2], F32)
        nc.vector.memset(warm[:], 0.0)
        nc.scalar.activation(out=warm[:, 1:2], in_=warm[:, 0:1], func=ACT.Relu)

        f_grp = keep.tile([P, ROWS, PACK], BF16, align_bytes=64)
        f_grp_words = f_grp[:].rearrange("p r t -> p (r t)").bitcast(F32).rearrange("p (r u) -> p r u", u=2)
        f_codes = keep.tile([P, ROWS], U32, align_bytes=64)
        f_scales = keep.tile([P, ROWS], U8, align_bytes=64)
        b_t = keep.tile([P, ROW_TILES, PACK, NODES, TILE_SETS], F32)
        a_ps = {}
        w1_sorted = keep.tile([P, 2, PACK, P], U32, align_bytes=64)
        w1_sorted_scales = keep.tile([P, 2, PACK, P], U8, align_bytes=64)

        def sort_words(g):
            nc.vector.tensor_copy(
                out=w1_sorted[:, g].bitcast(I32), in_=w1[:, g, :].bitcast(I32).rearrange("p (m t) -> p t m", t=PACK)
            )

        def sort_scales():
            nc.vector.tensor_copy(
                out=w1_sorted_scales[:], in_=w_planes[:, 0:2, :].rearrange("p g (m t) -> p g t m", t=PACK)
            )

        def prepare_codes(first, count=1):
            rows = slice(first * P, (first + count) * P)
            f_ps = banks.tile([P, 2, 2, P], F32, name="f_ps", tag="bank")
            for a in range(count):
                f_words = f_sb[:, first + a, :].bitcast(F32)
                for u in range(2):
                    nc.tensor.transpose(f_ps[:, a, u, :], f_words[:, u : C // 2 : 2], ident[:])
            nc.scalar.copy(
                out=f_grp_words[:, rows, :].rearrange("p (a r) u -> p a r u", a=count),
                in_=f_ps[:, 0:count].rearrange("p a u r -> p a r u"),
            )

        def quantise_rows(first, count=1):
            rows = slice(first * P, (first + count) * P)
            nc.vector.quantize_mx(
                out=f_codes[:, rows].bitcast(FP8X4),
                scales=f_scales[:, rows],
                in_=f_grp[:, rows, :].rearrange("p r t -> p (r t)"),
            )

        def multiply_rows(a, g, quarters):
            rows = slice(a * P, (a + 1) * P)
            for t in range(PACK):
                nc.tensor.matmul_mx(
                    out=quarters[t],
                    lhsT=w1_sorted[:, g, t].bitcast(FP8X4),
                    lhsT_scale=w1_sorted_scales[:, g, t],
                    rhs=f_codes[:, rows].bitcast(FP8X4),
                    rhs_scale=f_scales[:, rows],
                    start=True,
                    stop=True,
                )

        def quarters_of(bank):
            return [bank[:, t * P : (t + 1) * P] for t in range(PACK)]

        def prepare_products(a, shared=False):
            b_ps = banks.tile([P, C], F32, name="b_ps", tag="bank")
            quarters = quarters_of(b_ps)
            if shared:
                b_ps2 = banks.tile([P, C], F32, name="b_ps2", tag="bank")
                quarters = quarters[0:2] + quarters_of(b_ps2)[0:2]
            multiply_rows(a, 1, quarters)
            a_ps[a] = givers.tile([P, C], F32, name="a_ps", tag="a_ps")
            multiply_rows(a, 0, quarters_of(a_ps[a]))
            for t in range(PACK):
                by_j = quarters[t].rearrange("p (b j) -> p j b", j=NODES)
                if shared and t >= 2:
                    nc.vector.tensor_scalar_add(out=b_t[:, a, t], in0=by_j, scalar1=b1_pt[:, t : t + 1])
                else:
                    nc.scalar.activation(out=b_t[:, a, t], in_=by_j, func=ACT.Identity, bias=b1_pt[:, t : t + 1])

        b2_square = keep.tile([P, P], F32)
        b2_pos = keep.tile([P, OUT_TILES], F32)
        b2_sum = keep.tile([P, OUT_TILES], F32)
        b2_squares = keep.tile([P, OUT_TILES, P], F32)

        def spread_b2():
            nc.scalar.copy(out=b2_square[:], in_=b2_rows[:])
            b2_ps = banks.tile([P, C], F32, name="b2_ps", tag="bank")
            nc.tensor.transpose(b2_ps[:, 0:P], b2_square[:], ident[:])
            b2_cols = b2_ps[:, 0:OUT_TILES]
            nc.scalar.mul(out=b2_pos[:], in_=b2_cols, mul=POS_SLOPE)
            nc.scalar.mul(out=b2_sum[:], in_=b2_cols, mul=NODES * NEG_SLOPE)
            nc.scalar.copy(out=b2_squares[:], in_=b2_sum[:].unsqueeze(2).to_broadcast([P, OUT_TILES, P]))

        steps = []
        for a in range(ROW_TILES):
            j0 = 0
            for width in WIDTHS.get(a, [J_STEP] * STEPS_PER_TILE):
                steps.append((a, j0, width))
                j0 += width

        def split_of(s):
            return 0 if s == 0 or s >= len(steps) - ALONE else SHARE * steps[s][2] * P // 32 * PACK

        def width_of(s):
            return steps[s][2] * P * PACK
        v, h, v_bf, w_bf, codes, scales, r = {}, {}, {}, {}, {}, {}, {}
        pos_bank = {}
        lin, pos = {}, {}
        base = {}

        def add_pairs(s):
            a, j0, nj = steps[s]
            shape = [P, nj, TILE_SETS, NODES, PACK]
            v[s] = pairs.tile([P, V_WIDTH], F32, name="v", tag="v")
            nc.vector.tensor_tensor(
                out=v[s][:, 0 : width_of(s)].rearrange("p (j b i t) -> p j b i t", j=nj, b=TILE_SETS, i=NODES),
                in0=a_ps[a][:].rearrange("p (t b i) -> p b i t", t=PACK, i=NODES).unsqueeze(1).to_broadcast(shape),
                in1=b_t[:, a, :, j0 : j0 + nj].rearrange("p t j b -> p j b t").unsqueeze(3).to_broadcast(shape),
                op=ALU.add,
            )

        def leaky_by_vector(s):
            h[s] = pairs.tile([P, COLS * PACK], BF16, name="h", tag="h", align_bytes=64)
            nc.vector.scalar_tensor_tensor(
                out=h[s][:, split_of(s) : width_of(s)],
                in0=v[s][:, split_of(s) : width_of(s)],
                scalar=NEG_SLOPE,
                in1=v[s][:, split_of(s) : width_of(s)],
                op0=ALU.mult,
                op1=ALU.max,
            )

        def round_pairs(s):
            split = split_of(s)
            v_bf[s] = pairs.tile([P, split], BF16, name="v_bf", tag="v_bf")
            nc.scalar.copy(out=v_bf[s][:], in_=v[s][:, 0:split])

        def scale_pairs(s):
            split = split_of(s)
            if s == 1:
                w_bf[s] = h[0][:, 0:split]
            else:
                w_bf[s] = v[s][:].bitcast(BF16)[:, 2 * split : 3 * split]
            nc.gpsimd.tensor_scalar(
                out=w_bf[s], in0=v[s][:, 0:split], scalar1=NEG_SLOPE, scalar2=0.0, op0=ALU.mult, op1=ALU.add
            )

        def leaky_of_roundings(s):
            split = split_of(s)
            nc.vector.tensor_tensor(out=h[s][:, 0:split], in0=v_bf[s][:], in1=w_bf[s], op=ALU.max)

        def quantise(s):
            codes[s] = pairs.tile([P, COLS], U32, name="codes", tag="codes", align_bytes=64)
            scales[s] = pairs.tile([P, COLS], U8, name="scales", tag="scales", align_bytes=64)
            cols = steps[s][2] * P
            nc.vector.quantize_mx(
                out=codes[s][:, 0:cols].bitcast(FP8X4), scales=scales[s][:, 0:cols], in_=h[s][:, 0 : width_of(s)]
            )

        def multiply(s):
            a, j0, nj = steps[s]
            cols = nj * P
            x = []
            for n in range(OUT_TILES):
                chans = slice(n * P, (n + 1) * P)
                x.append(banks.tile([P, COLS], F32, name="x%d" % n, tag="bank"))
                nc.tensor.matmul_mx(
                    out=x[n][:, 0:cols],
                    lhsT=w2[:, chans].bitcast(FP8X4),
                    lhsT_scale=w_planes[:, 2, chans],
                    rhs=codes[s][:, 0:cols].bitcast(FP8X4),
                    rhs_scale=scales[s][:, 0:cols],
                    start=True,
                    stop=True,
                )
            if j0 == 0:
                lin[a] = groups.tile([P, C], F32, name="lin", tag="lin")
            for j in range(nj):
                cols = slice(j * P, (j + 1) * P)
                nc.tensor.matmul_mx(
                    out=lin[a][:],
                    lhsT=codes[s][:, cols].bitcast(FP8X4),
                    lhsT_scale=scales[s][:, cols],
                    rhs=w2[:].bitcast(FP8X4),
                    rhs_scale=w_planes[:, 2, :],
                    start=(j0 + j == 0),
                    stop=(j0 + j == NODES - 1),
                )
            return x

        def relu(s, x):
            r[s] = []
            for n in range(OUT_TILES):
                r[s].append(relus.tile([P, COLS], F32, name="r%d" % n, tag="r"))
                cols = steps[s][2] * P
                nc.scalar.activation(
                    out=r[s][n][:, 0:cols], in_=x[n][:, 0:cols], func=ACT.Relu, bias=b2_pos[:, n : n + 1], scale=POS_SLOPE
                )

        def add_up(s):
            a, j0, nj = steps[s]
            split = a == ROW_TILES - 1
            if j0 == 0:
                first = groups.tile([P, C], F32, name="pos", tag="pos")
                second = givers.tile([P, C], F32, name="pos_too", tag="a_ps") if split else first
                pos[a] = [(first if n < 2 else second)[:, n * P : (n + 1) * P] for n in range(OUT_TILES)]
                pos_bank[a] = [first, second]
                for n in range(OUT_TILES):
                    nc.tensor.matmul(
                        out=pos[a][n],
                        lhsT=b2_squares[:, n, :],
                        rhs=ident[:],
                        is_transpose=True,
                        start=(n == 0 or (split and n == 2)),
                        stop=False,
                    )
            for n in range(OUT_TILES):
                for j in range(nj):
                    nc.tensor.matmul(
                        out=pos[a][n],
                        lhsT=r[s][n][:, j * P : (j + 1) * P],
                        rhs=ident[:],
                        is_transpose=True,
                        start=False,
                        stop=(j0 + nj == NODES and j == nj - 1 and (n == OUT_TILES - 1 or (split and n == 1))),
                    )

        def scale_lin(a):
            base[a] = late.tile([P, C], F32, name="base", tag="base")
            nc.scalar.mul(out=base[a][:], in_=lin[a][:], mul=NEG_SLOPE)

        pos_sb = {}

        def take_pos(a):
            pos_sb[a] = late.tile([P, C], F32, name="pos_sb", tag="pos_sb")
            nc.scalar.copy(out=pos_sb[a][:], in_=pos_bank[a][0][:])

        def finish_late(a):
            result = stage.tile([P, C], F32, name="result", tag="result")
            nc.vector.tensor_tensor(out=result[:], in0=pos_sb[a][:], in1=base[a][:], op=ALU.add)
            nc.sync.dma_start(out=out_rows[a * P : (a + 1) * P, :], in_=result[:])

        def finish(a):
            result = stage.tile([P, C], F32, name="result", tag="result")
            for half in range(2):
                chans = slice(half * C // 2, (half + 1) * C // 2)
                nc.vector.tensor_tensor(
                    out=result[:, chans], in0=pos_bank[a][half][:, chans], in1=base[a][:, chans], op=ALU.add
                )
                nc.scalar.dma_start(out=out_rows[a * P : (a + 1) * P, chans], in_=result[:, chans])

        prepare_codes(0)
        sort_words(1)
        sort_scales()
        quantise_rows(0)
        sort_words(0)
        prepare_products(0, shared=True)
        spread_b2()
        prepare_codes(1)
        for a in range(2, ROW_TILES, 2):
            prepare_codes(a, 2)
        add_pairs(0)
        leaky_by_vector(0)
        add_pairs(1)
        quantise(0)
        round_pairs(1)

        for s in range(len(steps) + 1):
            a, j0, nj = steps[s] if s < len(steps) else (ROW_TILES, 0, 0)
            if 1 < s < len(steps) and steps[s - 2][0] < steps[s - 1][0]:
                take_pos(steps[s - 2][0])
            if s + 1 < len(steps) and split_of(s + 1):
                scale_pairs(s + 1)
            if s + LEAD < len(steps):
                add_pairs(s + LEAD)
            if s == 0:
                leaky_by_vector(1)
                quantise_rows(1)
            if s + 1 < len(steps) and split_of(s + 1):
                leaky_of_roundings(s + 1)
            deferred = s + LEAD < len(steps) and not split_of(s + LEAD)
            if s + LEAD < len(steps) and not deferred:
                leaky_by_vector(s + LEAD)
            if s + 1 < len(steps):
                quantise(s + 1)
            if deferred:
                leaky_by_vector(s + LEAD)
            if s < len(steps):
                relu(s, multiply(s))
            if s == 0:
                prepare_products(1)
            if a + AHEAD < ROW_TILES and j0 == J_STEP:
                if a % 2 == 0:
                    quantise_rows(a + AHEAD, 2)
            if a + AHEAD < ROW_TILES and j0 == 2 * J_STEP:
                prepare_products(a + AHEAD)
            if s == len(steps) - 1:
                add_up(s - 2)
            if s > 0 and s != len(steps) - 2:
                add_up(s - 1)
            if s < len(steps) and j0 + nj == NODES:
                scale_lin(a)
            if s + LEAD < len(steps) and split_of(s + LEAD):
                round_pairs(s + LEAD)
        for a in range(ROW_TILES - 1):
            finish_late(a)
        finish(ROW_TILES - 1)
